import numpy as np
import ml_dtypes


def mxq(x, axis, fmt="e4m3"):
    dtype, down = {"e4m3": (ml_dtypes.float8_e4m3fn, 7), "e5m2": (ml_dtypes.float8_e5m2, 14)}[fmt]
    v = np.moveaxis(np.asarray(x, np.float32).astype(ml_dtypes.bfloat16).astype(np.float64), axis, -1)
    blocks = v.reshape(v.shape[:-1] + (-1, 32))
    amax = np.abs(blocks).max(-1, keepdims=True)
    byte = np.maximum(np.where(amax > 0, np.frexp(amax)[1] - 1 + 127, 0) - down, 1)
    scale = np.exp2(byte - 127.0)
    codes = (blocks / scale).astype(np.float32).astype(dtype).astype(np.float64)
    return np.moveaxis((codes * scale).reshape(v.shape), -1, axis)


WIDE = False


def mx_kscale(k):
    if not WIDE:
        return np.ones(k)
    levels = np.array([10, -10, 5, -5, 0])
    a = np.random.permutation(np.resize(levels, k // 512 * 4)).reshape(k // 512, 4)
    idx = np.arange(k)
    return np.exp2(a[idx // 512, idx % 128 // 32])


BF16 = ml_dtypes.bfloat16


def bf(x):
    return np.asarray(x, np.float32).astype(BF16)


def f64(x):
    return np.asarray(x).astype(np.float64)


E2M1 = np.array([0.0, 0.5, 1.0, 1.5, 2.0, 3.0, 4.0, 6.0, -0.0, -0.5, -1.0, -1.5, -2.0, -3.0, -4.0, -6.0])


def pack_weight(w, fmt):
    k, n = w.shape
    w = f64(bf(w)).reshape(k // 32, 32, n)
    amax = np.abs(w).max(1)
    if fmt == "e4m3":
        byte = np.frexp(amax)[1] - 1 + 127 - 7
    else:
        mant, ex = np.frexp(amax / 6.0)
        byte = np.where(mant > 0.5, ex, ex - 1) + 127
    byte = np.clip(np.where(amax > 0, byte, 1), 1, 254)
    scaled = (w * np.exp2(127.0 - byte)[:, None, :]).reshape(k, n).astype(np.float32)
    by_word = np.ascontiguousarray(scaled.reshape(k // 512, 128, 4, n).transpose(0, 1, 3, 2))
    if fmt == "e4m3":
        words = by_word.astype(ml_dtypes.float8_e4m3fn).view(np.uint8)
    else:
        c = by_word.astype(ml_dtypes.float4_e2m1fn).view(np.uint8) & 0xF
        words = c[..., 0::2] | (c[..., 1::2] << 4)
    return np.ascontiguousarray(words), np.ascontiguousarray(byte.astype(np.uint8).reshape(k // 512, 16, n))


def unpack_weight(words, scales, fmt):
    g, p, n, _ = words.shape
    if fmt == "e4m3":
        vals = np.ascontiguousarray(words).view(ml_dtypes.float8_e4m3fn).astype(np.float64)
    else:
        nib = np.empty((g, p, n, 4), np.uint8)
        nib[..., 0::2] = words & 0xF
        nib[..., 1::2] = words >> 4
        vals = E2M1[nib]
    vals = vals * np.repeat(np.exp2(scales.astype(np.float64) - 127.0), 8, axis=1)[..., None]
    return vals.transpose(0, 1, 3, 2).reshape(g * 512, n)


B, T, C = 8, 512, 512
EPS = 1e-8
FMT = "e4m3"


def sigmoid(z):
    return 1.0 / (1.0 + np.exp(-z))


def setup_inputs():
    s = mx_kscale(C)
    t = mx_kscale(C)
    g = 1.0 / np.sqrt(C)
    x = bf(np.random.standard_normal((B, T, C)) * s)
    a0 = bf(np.random.standard_normal((B, C)) * t)
    b0 = bf(0.5 + np.random.uniform(size=(B, C)))
    x_prev0 = bf(np.random.standard_normal((B, C)) * s)
    w = bf((0.5 + 2.0 * np.random.uniform(size=C)) / T)
    u = bf(np.random.standard_normal(C) * 0.5)
    mu_r = bf(np.random.uniform(size=C))
    mu_k = bf(np.random.uniform(size=C))
    mu_v = bf(np.random.uniform(size=C))
    W_r_words, W_r_scales = pack_weight(np.ascontiguousarray((np.random.standard_normal((C, C)) * g / s[None, :]).T), FMT)
    W_k_words, W_k_scales = pack_weight(np.ascontiguousarray((np.random.standard_normal((C, C)) * g / s[None, :]).T), FMT)
    W_v_words, W_v_scales = pack_weight(np.ascontiguousarray((np.random.standard_normal((C, C)) * g / s[None, :] * t[:, None]).T), FMT)
    W_out_words, W_out_scales = pack_weight(np.ascontiguousarray((np.random.standard_normal((C, C)) * 2.0 * g / t[None, :]).T), FMT)
    return {
        "x": x,
        "a0": a0,
        "b0": b0,
        "x_prev0": x_prev0,
        "w": w,
        "u": u,
        "mu_r": mu_r,
        "mu_k": mu_k,
        "mu_v": mu_v,
        "W_r_words": W_r_words,
        "W_r_scales": W_r_scales,
        "W_k_words": W_k_words,
        "W_k_scales": W_k_scales,
        "W_v_words": W_v_words,
        "W_v_scales": W_v_scales,
        "W_out_words": W_out_words,
        "W_out_scales": W_out_scales,
    }


def reference(x, a0, b0, x_prev0, w, u, mu_r, mu_k, mu_v, W_r_words, W_r_scales, W_k_words, W_k_scales, W_v_words, W_v_scales, W_out_words, W_out_scales):
    x, a0, b0, x_prev0 = f64(x), f64(a0), f64(b0), f64(x_prev0)
    w, u = f64(w), f64(u)
    mu_r, mu_k, mu_v = f64(mu_r), f64(mu_k), f64(mu_v)
    x_shift = np.concatenate([x_prev0[:, None, :], x[:, :-1, :]], axis=1)
    xr = mu_r * x + (1.0 - mu_r) * x_shift
    xk = mu_k * x + (1.0 - mu_k) * x_shift
    xv = mu_v * x + (1.0 - mu_v) * x_shift
    r = sigmoid(mxq(xr, 2, "e4m3") @ unpack_weight(W_r_words, W_r_scales, FMT))
    k = mxq(xk, 2, "e4m3") @ unpack_weight(W_k_words, W_k_scales, FMT)
    v = mxq(xv, 2, "e4m3") @ unpack_weight(W_v_words, W_v_scales, FMT)
    ek = np.exp(u + k)
    steps = np.arange(1, T + 1).astype(np.float64)
    decay_pow = np.exp(-w[None, :] * steps[:, None])
    a_t = a0[:, None, :] * decay_pow[None]
    b_t = b0[:, None, :] * decay_pow[None]
    wkv = (a_t + ek * v) / (b_t + ek + EPS)
    h = r * wkv
    return mxq(h, 2, "e4m3") @ unpack_weight(W_out_words, W_out_scales, FMT)

@@ -1,0 +1,294 @@
+import math
+from contextlib import ExitStack
+
+import concourse.mybir as mybir
+from concourse.masks import make_identity
+
+F32 = mybir.dt.float32
+BF16 = mybir.dt.bfloat16
+I32 = mybir.dt.int32
+U32 = mybir.dt.uint32
+U8 = mybir.dt.uint8
+FP8X4 = mybir.dt.float8_e4m3fn_x4
+ALU = mybir.AluOpType
+ACT = mybir.ActivationFunctionType
+
+P = 128
+PACK = 4
+B, T, C = 8, 512, 512
+CH_TILES = C // P
+TOK_TILES = T // P
+HALF = T // 2
+EPS = 1e-8
+
+FLOPS = 4 * 2 * B * T * C * C
+
+ROW_A0 = 0
+ROW_B0 = 8
+ROW_XPREV = 16
+ROW_W = 24
+ROW_U = 25
+ROW_MU = 26
+ROWS = 32
+
+W_R, W_K, W_V, W_OUT = 0, 1, 2, 3
+
+
+def tile_rwkv_timemix_pa_t_kernel(
+    tc,
+    x,
+    a0,
+    b0,
+    x_prev0,
+    w,
+    u,
+    mu_r,
+    mu_k,
+    mu_v,
+    W_r_words,
+    W_r_scales,
+    W_k_words,
+    W_k_scales,
+    W_v_words,
+    W_v_scales,
+    W_out_words,
+    W_out_scales,
+    out,
+):
+    nc = tc.nc
+    with ExitStack() as stack:
+        const = stack.enter_context(tc.tile_pool(name="const", bufs=1))
+        front = stack.enter_context(tc.tile_pool(name="front", bufs=2))
+        back = stack.enter_context(tc.tile_pool(name="back", bufs=2))
+        psum = stack.enter_context(tc.psum_pool(name="psum", bufs=1))
+
+        rows = const.tile([P, C], BF16)
+        nc.vector.memset(rows[:], 0.0)
+        nc.sync.dma_start(out=rows[ROW_A0 : ROW_A0 + B, :], in_=a0)
+        nc.sync.dma_start(out=rows[ROW_B0 : ROW_B0 + B, :], in_=b0)
+        nc.sync.dma_start(out=rows[ROW_XPREV : ROW_XPREV + B, :], in_=x_prev0)
+        for row, vector in ((ROW_W, w), (ROW_U, u), (ROW_MU, mu_r), (ROW_MU + 1, mu_k), (ROW_MU + 2, mu_v)):
+            nc.sync.dma_start(out=rows[row : row + 1, :], in_=vector.unsqueeze(0))
+
+        def load_x(b):
+            x_sb = front.tile([P, TOK_TILES, C], BF16, tag="x_sb")
+            nc.sync.dma_start(out=x_sb[:], in_=x[b].rearrange("(i p) c -> p i c", p=P))
+            return x_sb
+
+        x_first = load_x(0)
+
+        w_codes = const.tile([P, 4, PACK * C], U8, align_bytes=64)
+        w_planes = const.tile([P, 4, C], U8, align_bytes=64)
+        nc.vector.memset(w_planes[:].rearrange("p w n -> p (w n)").bitcast(I32), 0)
+        weights = (
+            (W_r_words, W_r_scales),
+            (W_k_words, W_k_scales),
+            (W_v_words, W_v_scales),
+            (W_out_words, W_out_scales),
+        )
+        for wi, (words, scales) in enumerate(weights):
+            nc.sync.dma_start(
+                out=w_codes[:, wi, :].bitcast(I32),
+                in_=words[0].rearrange("p n t -> p (n t)").bitcast(I32),
+            )
+            for quadrant in range(4):
+                nc.sync.dma_start(
+                    out=w_planes[32 * quadrant : 32 * quadrant + 4, wi, :].bitcast(I32),
+                    in_=scales[0, 4 * quadrant : 4 * quadrant + 4, :].bitcast(I32),
+                )
+
+        ident_f32 = const.tile([P, P], F32)
+        make_identity(nc, ident_f32[:])
+        ident_bf16 = const.tile([P, P], BF16)
+        make_identity(nc, ident_bf16[:])
+
+        rows_t = psum.tile([P, 2 * CH_TILES, P], BF16, tag="xt")
+        for j in range(CH_TILES):
+            nc.tensor.transpose(rows_t[:, j, :], rows[:, P * j : P * (j + 1)], ident_bf16[:])
+        for t in range(PACK):
+            nc.tensor.transpose(rows_t[:, CH_TILES + t, :], rows[:, t:C:PACK], ident_bf16[:])
+        cols = const.tile([P, 2 * CH_TILES, ROWS], F32)
+        nc.vector.tensor_copy(out=cols[:], in_=rows_t[:, :, 0:ROWS])
+        by_tile = cols[:, 0:CH_TILES, :]
+        by_word = cols[:, CH_TILES : CH_TILES + PACK, :]
+        a0_col = by_tile[:, :, ROW_A0 : ROW_A0 + B]
+        b0_col = by_tile[:, :, ROW_B0 : ROW_B0 + B]
+
+        def mix_and_quantise(b, x_sb):
+            xg = front.tile([P, T + 1, PACK], BF16, tag="xg")
+            xg_words = (
+                xg[:].rearrange("p k t -> p (k t)").bitcast(F32).rearrange("p (k pair) -> p k pair", pair=2)
+            )
+            nc.scalar.copy(out=xg[:, 0, :], in_=by_word[:, :, ROW_XPREV + b])
+            for half in range(2):
+                xt = psum.tile([P, 2, HALF], F32, tag="xt")
+                for pair in range(2):
+                    for i in range(2):
+                        nc.tensor.transpose(
+                            xt[:, pair, P * i : P * (i + 1)],
+                            x_sb[:, 2 * half + i, :].bitcast(F32)[:, pair : C // 2 : 2],
+                            ident_f32[:],
+                        )
+                nc.scalar.copy(
+                    out=xg_words[:, 1 + HALF * half : 1 + HALF * (half + 1), :],
+                    in_=xt[:].rearrange("p pair k -> p k pair"),
+                )
+
+            xg_flat = xg[:].rearrange("p k t -> p (k t)")
+            step = front.tile([P, T, PACK], F32, tag="step")
+            nc.vector.tensor_sub(
+                out=step[:].rearrange("p k t -> p (k t)"),
+                in0=xg_flat[:, PACK : PACK * (T + 1)],
+                in1=xg_flat[:, 0 : PACK * T],
+            )
+            quantised = []
+            for mix in range(3):
+                scaled = front.tile([P, PACK, T], F32, tag="scaled")
+                for t in range(PACK):
+                    nc.scalar.activation(
+                        out=scaled[:, t, :],
+                        in_=step[:, :, t],
+                        func=ACT.Copy,
+                        scale=by_word[:, t, ROW_MU + mix : ROW_MU + mix + 1],
+                    )
+                mixed = front.tile([P, T, PACK], BF16, tag="mixed", bufs=3, align_bytes=64)
+                nc.vector.tensor_add(
+                    out=mixed[:], in0=scaled[:].rearrange("p t k -> p k t"), in1=xg[:, 0:T, :]
+                )
+                codes = front.tile([P, T], U32, tag="codes%d" % mix, align_bytes=64)
+                plane = front.tile([P, T], U8, tag="plane%d" % mix, align_bytes=64)
+                nc.vector.quantize_mx(
+                    out=codes[:].bitcast(FP8X4),
+                    scales=plane[:],
+                    in_=mixed[:].rearrange("p k t -> p (k t)"),
+                )
+                quantised.append((codes, plane))
+            return quantised
+
+        mixes_next = mix_and_quantise(0, x_first)
+
+        neg_alpha = const.tile([P, CH_TILES, B], F32)
+        chi_bias = const.tile([P, CH_TILES, B], F32)
+        b0_inverse = const.tile([P, CH_TILES, B], F32)
+        nc.vector.reciprocal(b0_inverse[:], b0_col)
+        nc.vector.scalar_tensor_tensor(
+            out=neg_alpha[:], in0=a0_col, scalar=-1.0, in1=b0_inverse[:], op0=ALU.mult, op1=ALU.mult
+        )
+        eps_col = const.tile([P, 1], F32)
+        nc.vector.memset(eps_col[:], EPS)
+
+        steps_i32 = back.tile([P, T], I32, tag="o_sb", bufs=4)
+        nc.gpsimd.iota(steps_i32[:], pattern=[[1, T]], base=1, channel_multiplier=0)
+        steps = back.tile([P, T], F32, tag="o_sb", bufs=4)
+        nc.vector.tensor_copy(out=steps[:], in_=steps_i32[:])
+        w_steps = const.tile([P, CH_TILES, T], F32)
+        for j in range(CH_TILES):
+            nc.vector.tensor_scalar_mul(
+                out=w_steps[:, j, :], in0=steps[:], scalar1=by_tile[:, j, ROW_W : ROW_W + 1]
+            )
+        decay = back.tile([P, CH_TILES, T], F32, tag="h_planes")
+        nc.scalar.activation(out=decay[:], in_=w_steps[:], func=ACT.Exp, scale=-1.0)
+
+        ln_b0 = const.tile([P, CH_TILES, B], F32)
+        nc.scalar.activation(out=ln_b0[:], in_=b0_col, func=ACT.Ln)
+        nc.vector.tensor_scalar_add(out=chi_bias[:], in0=ln_b0[:], scalar1=-math.log(EPS))
+        ln_beta = const.tile([P, B, CH_TILES, T], F32)
+        for b in range(B):
+            for j in range(CH_TILES):
+                nc.scalar.activation(
+                    out=ln_beta[:, b, j, :],
+                    in_=decay[:, j, :],
+                    func=ACT.Ln,
+                    scale=b0_col[:, j, b : b + 1],
+                    bias=eps_col[:],
+                )
+
+        def stage1(mixes, which, j, tag, bufs):
+            codes, plane = mixes[which]
+            acc = psum.tile([P, T], F32, tag=tag, bufs=bufs)
+            nc.tensor.matmul_mx(
+                out=acc[:],
+                lhsT=w_codes[:, which, PACK * P * j : PACK * P * (j + 1)].bitcast(FP8X4),
+                lhsT_scale=w_planes[:, which, P * j : P * (j + 1)],
+                rhs=codes[:].bitcast(FP8X4),
+                rhs_scale=plane[:],
+                start=True,
+                stop=True,
+            )
+            return acc
+
+        for b in range(B):
+            mixes = mixes_next
+            if b + 1 < B:
+                mixes_next = mix_and_quantise(b + 1, load_x(b + 1))
+
+            for j in range(CH_TILES):
+                k_acc = stage1(mixes, W_K, j, "k", 2)
+                v_acc = stage1(mixes, W_V, j, "v", 2)
+                r_acc = stage1(mixes, W_R, j, "r", 1)
+
+                chi = back.tile([P, T], F32, tag="chi")
+                nc.scalar.activation(
+                    out=chi[:],
+                    in_=w_steps[:, j, :],
+                    func=ACT.Sigmoid,
+                    scale=-1.0,
+                    bias=chi_bias[:, j, b : b + 1],
+                )
+                logit = back.tile([P, T], F32, tag="logit")
+                nc.vector.tensor_sub(out=logit[:], in0=k_acc[:], in1=ln_beta[:, b, j, :])
+                s = back.tile([P, T], F32, tag="s")
+                nc.scalar.activation(
+                    out=s[:], in_=logit[:], func=ACT.Sigmoid, bias=by_tile[:, j, ROW_U : ROW_U + 1]
+                )
+                r = back.tile([P, T], F32, tag="r")
+                nc.scalar.activation(out=r[:], in_=r_acc[:], func=ACT.Sigmoid)
+
+                state_share = back.tile([P, T], F32, tag="state_share")
+                nc.vector.scalar_tensor_tensor(
+                    out=state_share[:], in0=s[:], scalar=-1.0, in1=chi[:], op0=ALU.add, op1=ALU.mult
+                )
+                sv = back.tile([P, T], F32, tag="sv")
+                nc.vector.tensor_mul(out=sv[:], in0=s[:], in1=v_acc[:])
+                wkv = back.tile([P, T], F32, tag="wkv")
+                nc.vector.scalar_tensor_tensor(
+                    out=wkv[:],
+                    in0=state_share[:],
+                    scalar=neg_alpha[:, j, b : b + 1],
+                    in1=sv[:],
+                    op0=ALU.mult,
+                    op1=ALU.add,
+                )
+                h = back.tile([P, T], F32, tag="h")
+                nc.vector.tensor_mul(out=h[:], in0=wkv[:], in1=r[:])
+                nc.sync.dma_start(out=out[b, P * j : P * (j + 1), :], in_=h[:])
+
+            h_planes = back.tile([P, PACK, T], F32, tag="h_planes")
+            nc.sync.dma_start(out=h_planes[:], in_=out[b].rearrange("(p t) k -> p t k", t=PACK))
+            h_words = back.tile([P, T, PACK], BF16, tag="h_words", align_bytes=64)
+            nc.scalar.copy(out=h_words[:], in_=h_planes[:].rearrange("p t k -> p k t"))
+            h_codes = back.tile([P, T], U32, tag="h_codes", align_bytes=64)
+            h_plane = back.tile([P, T], U8, tag="h_plane", align_bytes=64)
+            nc.vector.quantize_mx(
+                out=h_codes[:].bitcast(FP8X4),
+                scales=h_plane[:],
+                in_=h_words[:].rearrange("p k t -> p (k t)"),
+            )
+
+            for i in range(TOK_TILES):
+                o_acc = psum.tile([P, C], F32, tag="o", bufs=2)
+                nc.tensor.matmul_mx(
+                    out=o_acc[:],
+                    lhsT=h_codes[:, P * i : P * (i + 1)].bitcast(FP8X4),
+                    lhsT_scale=h_plane[:, P * i : P * (i + 1)],
+                    rhs=w_codes[:, W_OUT, :].bitcast(FP8X4),
+                    rhs_scale=w_planes[:, W_OUT, :],
+                    start=True,
+                    stop=True,
+                )
+                o_sb = back.tile([P, C], F32, tag="o_sb", bufs=4)
+                if i % 2 == 0:
+                    nc.scalar.copy(out=o_sb[:], in_=o_acc[:])
+                else:
+                    nc.vector.tensor_copy(out=o_sb[:], in_=o_acc[:])
+                nc.sync.dma_start(out=out[b, P * i : P * (i + 1), :], in_=o_sb[:])

@@ -18,7 +18,6 @@ PACK = 4
 B, T, C = 8, 512, 512
 CH_TILES = C // P
 TOK_TILES = T // P
-HALF = T // 2
 EPS = 1e-8
 
 FLOPS = 4 * 2 * B * T * C * C
@@ -97,8 +96,6 @@ def tile_rwkv_timemix_pa_t_kernel(
                     in_=scales[0, 4 * quadrant : 4 * quadrant + 4, :].bitcast(I32),
                 )
 
-        ident_f32 = const.tile([P, P], F32)
-        make_identity(nc, ident_f32[:])
         ident_bf16 = const.tile([P, P], BF16)
         make_identity(nc, ident_bf16[:])
 
@@ -114,47 +111,44 @@ def tile_rwkv_timemix_pa_t_kernel(
         a0_col = by_tile[:, :, ROW_A0 : ROW_A0 + B]
         b0_col = by_tile[:, :, ROW_B0 : ROW_B0 + B]
 
-        def mix_and_quantise(b, x_sb):
-            xg = front.tile([P, T + 1, PACK], BF16, tag="xg")
-            xg_words = (
-                xg[:].rearrange("p k t -> p (k t)").bitcast(F32).rearrange("p (k pair) -> p k pair", pair=2)
+        def regroup(dst, planes):
+            nc.scalar.copy(
+                out=dst.rearrange("p (c i) t -> p c t i", i=4),
+                in_=planes.rearrange("p t (c i) -> p c t i", i=4),
             )
-            nc.scalar.copy(out=xg[:, 0, :], in_=by_word[:, :, ROW_XPREV + b])
-            for half in range(2):
-                xt = psum.tile([P, 2, HALF], F32, tag="xt")
-                for pair in range(2):
-                    for i in range(2):
-                        nc.tensor.transpose(
-                            xt[:, pair, P * i : P * (i + 1)],
-                            x_sb[:, 2 * half + i, :].bitcast(F32)[:, pair : C // 2 : 2],
-                            ident_f32[:],
-                        )
-                nc.scalar.copy(
-                    out=xg_words[:, 1 + HALF * half : 1 + HALF * (half + 1), :],
-                    in_=xt[:].rearrange("p pair k -> p k pair"),
-                )
 
-            xg_flat = xg[:].rearrange("p k t -> p (k t)")
-            step = front.tile([P, T, PACK], F32, tag="step")
+        def mix_and_quantise(b, x_sb):
+            x_planes = front.tile([P, PACK, T + 2], BF16, tag="x_planes")
+            nc.scalar.copy(out=x_planes[:, :, 1], in_=by_word[:, :, ROW_XPREV + b])
+            for pair in range(2):
+                xt = psum.tile([P, 2, T], BF16, tag="xt")
+                for e in range(2):
+                    for i in range(TOK_TILES):
+                        nc.tensor.transpose(
+                            xt[:, e, P * i : P * (i + 1)],
+                            x_sb[:, i, 2 * pair + e : C : PACK],
+                            ident_bf16[:],
+                        )
+                nc.scalar.copy(out=x_planes[:, 2 * pair : 2 * pair + 2, 2 : T + 2], in_=xt[:])
+
+            step = front.tile([P, PACK, T], F32, tag="step")
             nc.vector.tensor_sub(
-                out=step[:].rearrange("p k t -> p (k t)"),
-                in0=xg_flat[:, PACK : PACK * (T + 1)],
-                in1=xg_flat[:, 0 : PACK * T],
+                out=step[:], in0=x_planes[:, :, 2 : T + 2], in1=x_planes[:, :, 1 : T + 1]
             )
             quantised = []
             for mix in range(3):
-                scaled = front.tile([P, PACK, T], F32, tag="scaled")
+                mixed_planes = front.tile([P, PACK, T], BF16, tag="mixed_planes")
                 for t in range(PACK):
-                    nc.scalar.activation(
-                        out=scaled[:, t, :],
-                        in_=step[:, :, t],
-                        func=ACT.Copy,
-                        scale=by_word[:, t, ROW_MU + mix : ROW_MU + mix + 1],
+                    nc.vector.scalar_tensor_tensor(
+                        out=mixed_planes[:, t, :],
+                        in0=step[:, t, :],
+                        scalar=by_word[:, t, ROW_MU + mix : ROW_MU + mix + 1],
+                        in1=x_planes[:, t, 1 : T + 1],
+                        op0=ALU.mult,
+                        op1=ALU.add,
                     )
-                mixed = front.tile([P, T, PACK], BF16, tag="mixed", bufs=3, align_bytes=64)
-                nc.vector.tensor_add(
-                    out=mixed[:], in0=scaled[:].rearrange("p t k -> p k t"), in1=xg[:, 0:T, :]
-                )
+                mixed = front.tile([P, T, PACK], BF16, tag="mixed", align_bytes=64)
+                regroup(mixed[:], mixed_planes[:])
                 codes = front.tile([P, T], U32, tag="codes%d" % mix, align_bytes=64)
                 plane = front.tile([P, T], U8, tag="plane%d" % mix, align_bytes=64)
                 nc.vector.quantize_mx(
@@ -227,7 +221,7 @@ def tile_rwkv_timemix_pa_t_kernel(
                 v_acc = stage1(mixes, W_V, j, "v", 2)
                 r_acc = stage1(mixes, W_R, j, "r", 1)
 
-                chi = back.tile([P, T], F32, tag="chi")
+                chi = back.tile([P, T], F32, tag="chi", bufs=3)
                 nc.scalar.activation(
                     out=chi[:],
                     in_=w_steps[:, j, :],
@@ -235,13 +229,13 @@ def tile_rwkv_timemix_pa_t_kernel(
                     scale=-1.0,
                     bias=chi_bias[:, j, b : b + 1],
                 )
-                logit = back.tile([P, T], F32, tag="logit")
+                logit = back.tile([P, T], F32, tag="logit", bufs=3)
                 nc.vector.tensor_sub(out=logit[:], in0=k_acc[:], in1=ln_beta[:, b, j, :])
-                s = back.tile([P, T], F32, tag="s")
+                s = back.tile([P, T], F32, tag="s", bufs=3)
                 nc.scalar.activation(
                     out=s[:], in_=logit[:], func=ACT.Sigmoid, bias=by_tile[:, j, ROW_U : ROW_U + 1]
                 )
-                r = back.tile([P, T], F32, tag="r")
+                r = back.tile([P, T], F32, tag="r", bufs=3)
                 nc.scalar.activation(out=r[:], in_=r_acc[:], func=ACT.Sigmoid)
 
                 state_share = back.tile([P, T], F32, tag="state_share")
@@ -266,7 +260,7 @@ def tile_rwkv_timemix_pa_t_kernel(
             h_planes = back.tile([P, PACK, T], F32, tag="h_planes")
             nc.sync.dma_start(out=h_planes[:], in_=out[b].rearrange("(p t) k -> p t k", t=PACK))
             h_words = back.tile([P, T, PACK], BF16, tag="h_words", align_bytes=64)
-            nc.scalar.copy(out=h_words[:], in_=h_planes[:].rearrange("p t k -> p k t"))
+            regroup(h_words[:], h_planes[:])
             h_codes = back.tile([P, T], U32, tag="h_codes", align_bytes=64)
             h_plane = back.tile([P, T], U8, tag="h_plane", align_bytes=64)
             nc.vector.quantize_mx(
@@ -287,8 +281,5 @@ def tile_rwkv_timemix_pa_t_kernel(
                     stop=True,
                 )
                 o_sb = back.tile([P, C], F32, tag="o_sb", bufs=4)
-                if i % 2 == 0:
-                    nc.scalar.copy(out=o_sb[:], in_=o_acc[:])
-                else:
-                    nc.vector.tensor_copy(out=o_sb[:], in_=o_acc[:])
+                nc.scalar.copy(out=o_sb[:], in_=o_acc[:])
                 nc.sync.dma_start(out=out[b, P * i : P * (i + 1), :], in_=o_sb[:])

@@ -32,6 +32,11 @@ ROWS = 32
 
 W_R, W_K, W_V, W_OUT = 0, 1, 2, 3
 
+UNITS = B * CH_TILES
+FIRST_STEP = -13
+LAST_STEP = UNITS + 5
+LN_FIRST_STEP = -B - 1
+
 
 def tile_rwkv_timemix_pa_t_kernel(
     tc,
@@ -61,6 +66,8 @@ def tile_rwkv_timemix_pa_t_kernel(
         back = stack.enter_context(tc.tile_pool(name="back", bufs=2))
         psum = stack.enter_context(tc.psum_pool(name="psum", bufs=1))
 
+        stack.enter_context(tc.manual_schedule())
+
         rows = const.tile([P, C], BF16)
         nc.vector.memset(rows[:], 0.0)
         nc.sync.dma_start(out=rows[ROW_A0 : ROW_A0 + B, :], in_=a0)
@@ -68,13 +75,6 @@ def tile_rwkv_timemix_pa_t_kernel(
         nc.sync.dma_start(out=rows[ROW_XPREV : ROW_XPREV + B, :], in_=x_prev0)
         for row, vector in ((ROW_W, w), (ROW_U, u), (ROW_MU, mu_r), (ROW_MU + 1, mu_k), (ROW_MU + 2, mu_v)):
             nc.sync.dma_start(out=rows[row : row + 1, :], in_=vector.unsqueeze(0))
-
-        def load_x(b):
-            x_sb = front.tile([P, TOK_TILES, C], BF16, tag="x_sb")
-            nc.sync.dma_start(out=x_sb[:], in_=x[b].rearrange("(i p) c -> p i c", p=P))
-            return x_sb
-
-        x_first = load_x(0)
 
         w_codes = const.tile([P, 4, PACK * C], U8, align_bytes=64)
         w_planes = const.tile([P, 4, C], U8, align_bytes=64)
@@ -99,6 +99,12 @@ def tile_rwkv_timemix_pa_t_kernel(
         ident_bf16 = const.tile([P, P], BF16)
         make_identity(nc, ident_bf16[:])
 
+        difference = const.tile([P, P], BF16)
+        nc.vector.tensor_copy(out=difference[:], in_=ident_bf16[:])
+        nc.vector.tensor_sub(out=difference[:, 1:P], in0=difference[:, 1:P], in1=ident_bf16[:, 0 : P - 1])
+        neg_ident = const.tile([P, P], BF16)
+        nc.vector.tensor_scalar_mul(out=neg_ident[:], in0=ident_bf16[:], scalar1=-1.0)
+
         rows_t = psum.tile([P, 2 * CH_TILES, P], BF16, tag="xt")
         for j in range(CH_TILES):
             nc.tensor.transpose(rows_t[:, j, :], rows[:, P * j : P * (j + 1)], ident_bf16[:])
@@ -111,58 +117,21 @@ def tile_rwkv_timemix_pa_t_kernel(
         a0_col = by_tile[:, :, ROW_A0 : ROW_A0 + B]
         b0_col = by_tile[:, :, ROW_B0 : ROW_B0 + B]
 
-        def regroup(dst, planes):
-            nc.scalar.copy(
-                out=dst.rearrange("p (c i) t -> p c t i", i=4),
-                in_=planes.rearrange("p t (c i) -> p c t i", i=4),
+        counts_i32 = back.tile([P, T], I32, tag="o_sb")
+        nc.gpsimd.iota(counts_i32[:], pattern=[[1, T]], base=1, channel_multiplier=0)
+        counts = back.tile([P, T], F32, tag="o_sb")
+        nc.vector.tensor_copy(out=counts[:], in_=counts_i32[:])
+        w_steps = const.tile([P, CH_TILES, T], F32)
+        for j in range(CH_TILES):
+            nc.vector.tensor_scalar_mul(
+                out=w_steps[:, j, :], in0=counts[:], scalar1=by_tile[:, j, ROW_W : ROW_W + 1]
             )
-
-        def mix_and_quantise(b, x_sb):
-            x_planes = front.tile([P, PACK, T + 2], BF16, tag="x_planes")
-            nc.scalar.copy(out=x_planes[:, :, 1], in_=by_word[:, :, ROW_XPREV + b])
-            for pair in range(2):
-                xt = psum.tile([P, 2, T], BF16, tag="xt")
-                for e in range(2):
-                    for i in range(TOK_TILES):
-                        nc.tensor.transpose(
-                            xt[:, e, P * i : P * (i + 1)],
-                            x_sb[:, i, 2 * pair + e : C : PACK],
-                            ident_bf16[:],
-                        )
-                nc.scalar.copy(out=x_planes[:, 2 * pair : 2 * pair + 2, 2 : T + 2], in_=xt[:])
-
-            step = front.tile([P, PACK, T], F32, tag="step")
-            nc.vector.tensor_sub(
-                out=step[:], in0=x_planes[:, :, 2 : T + 2], in1=x_planes[:, :, 1 : T + 1]
-            )
-            quantised = []
-            for mix in range(3):
-                mixed_planes = front.tile([P, PACK, T], BF16, tag="mixed_planes")
-                for t in range(PACK):
-                    nc.vector.scalar_tensor_tensor(
-                        out=mixed_planes[:, t, :],
-                        in0=step[:, t, :],
-                        scalar=by_word[:, t, ROW_MU + mix : ROW_MU + mix + 1],
-                        in1=x_planes[:, t, 1 : T + 1],
-                        op0=ALU.mult,
-                        op1=ALU.add,
-                    )
-                mixed = front.tile([P, T, PACK], BF16, tag="mixed", align_bytes=64)
-                regroup(mixed[:], mixed_planes[:])
-                codes = front.tile([P, T], U32, tag="codes%d" % mix, align_bytes=64)
-                plane = front.tile([P, T], U8, tag="plane%d" % mix, align_bytes=64)
-                nc.vector.quantize_mx(
-                    out=codes[:].bitcast(FP8X4),
-                    scales=plane[:],
-                    in_=mixed[:].rearrange("p k t -> p (k t)"),
-                )
-                quantised.append((codes, plane))
-            return quantised
-
-        mixes_next = mix_and_quantise(0, x_first)
+        decay = back.tile([P, CH_TILES, T], F32, tag="h_planes")
+        nc.scalar.activation(out=decay[:], in_=w_steps[:], func=ACT.Exp, scale=-1.0)
+        chi_bias = const.tile([P, CH_TILES, B], F32)
+        nc.scalar.activation(out=chi_bias[:], in_=b0_col, func=ACT.Ln, scale=1.0 / EPS)
 
         neg_alpha = const.tile([P, CH_TILES, B], F32)
-        chi_bias = const.tile([P, CH_TILES, B], F32)
         b0_inverse = const.tile([P, CH_TILES, B], F32)
         nc.vector.reciprocal(b0_inverse[:], b0_col)
         nc.vector.scalar_tensor_tensor(
@@ -170,38 +139,110 @@ def tile_rwkv_timemix_pa_t_kernel(
         )
         eps_col = const.tile([P, 1], F32)
         nc.vector.memset(eps_col[:], EPS)
-
-        steps_i32 = back.tile([P, T], I32, tag="o_sb", bufs=4)
-        nc.gpsimd.iota(steps_i32[:], pattern=[[1, T]], base=1, channel_multiplier=0)
-        steps = back.tile([P, T], F32, tag="o_sb", bufs=4)
-        nc.vector.tensor_copy(out=steps[:], in_=steps_i32[:])
-        w_steps = const.tile([P, CH_TILES, T], F32)
-        for j in range(CH_TILES):
-            nc.vector.tensor_scalar_mul(
-                out=w_steps[:, j, :], in0=steps[:], scalar1=by_tile[:, j, ROW_W : ROW_W + 1]
-            )
-        decay = back.tile([P, CH_TILES, T], F32, tag="h_planes")
-        nc.scalar.activation(out=decay[:], in_=w_steps[:], func=ACT.Exp, scale=-1.0)
-
-        ln_b0 = const.tile([P, CH_TILES, B], F32)
-        nc.scalar.activation(out=ln_b0[:], in_=b0_col, func=ACT.Ln)
-        nc.vector.tensor_scalar_add(out=chi_bias[:], in0=ln_b0[:], scalar1=-math.log(EPS))
         ln_beta = const.tile([P, B, CH_TILES, T], F32)
-        for b in range(B):
+
+        def make_ln_beta(q):
             for j in range(CH_TILES):
                 nc.scalar.activation(
-                    out=ln_beta[:, b, j, :],
+                    out=ln_beta[:, q, j, :],
                     in_=decay[:, j, :],
                     func=ACT.Ln,
-                    scale=b0_col[:, j, b : b + 1],
+                    scale=b0_col[:, j, q : q + 1],
                     bias=eps_col[:],
                 )
 
-        def stage1(mixes, which, j, tag, bufs):
-            codes, plane = mixes[which]
-            acc = psum.tile([P, T], F32, tag=tag, bufs=bufs)
+        x_rows, x_planes, steps, mixed_planes, mixed, mixes = {}, {}, {}, {}, {}, {}
+
+        def copy(on_vector, dst, src):
+            if on_vector:
+                nc.vector.tensor_copy(out=dst, in_=src)
+            else:
+                nc.scalar.copy(out=dst, in_=src)
+
+        def load_x(f):
+            x_rows[f] = front.tile([P, TOK_TILES, C], BF16, tag="x_rows", name="x_rows")
+            nc.sync.dma_start(out=x_rows[f][:], in_=x[f].rearrange("(i p) c -> p i c", p=P))
+
+        def transpose_x(f, pair, on_vector):
+            if pair == 0:
+                x_planes[f] = front.tile([P, PACK, T + 2], BF16, tag="x_planes", name="x_planes")
+                copy(on_vector, x_planes[f][:, :, 1], by_word[:, :, ROW_XPREV + f])
+            xt = psum.tile([P, 2, T], BF16, tag="xt")
+            for e in range(2):
+                for i in range(TOK_TILES):
+                    nc.tensor.transpose(
+                        xt[:, e, P * i : P * (i + 1)],
+                        x_rows[f][:, i, 2 * pair + e : C : PACK],
+                        ident_bf16[:],
+                    )
+            copy(on_vector, x_planes[f][:, 2 * pair : 2 * pair + 2, 2 : T + 2], xt[:])
+
+        def difference_plane(f, t):
+            steps[f, t] = psum.tile([P, T], F32, tag="step", name="step", bufs=2)
+            for i in range(TOK_TILES):
+                nc.tensor.matmul(
+                    out=steps[f, t][:, P * i : P * (i + 1)],
+                    lhsT=x_rows[f][:, i, t:C:PACK],
+                    rhs=difference[:],
+                    start=True,
+                    stop=False,
+                )
+                if i == 0:
+                    before, row = rows, ROW_XPREV + f
+                else:
+                    before, row = x_rows[f][:, i - 1, :], P - 1
+                nc.tensor.matmul(
+                    out=steps[f, t][:, P * i : P * i + 1],
+                    lhsT=before[:, t:C:PACK],
+                    rhs=neg_ident[:, row : row + 1],
+                    start=False,
+                    stop=True,
+                )
+
+        def mix_plane(f, t):
+            for mix in (W_K, W_V, W_R):
+                if t == 0:
+                    mixed_planes[f, mix] = front.tile(
+                        [P, PACK, T], BF16, tag="mixed_planes%d" % mix, name="mixed_planes"
+                    )
+                nc.vector.scalar_tensor_tensor(
+                    out=mixed_planes[f, mix][:, t, :],
+                    in0=steps[f, t][:],
+                    scalar=by_word[:, t, ROW_MU + mix : ROW_MU + mix + 1],
+                    in1=x_planes[f][:, t, 1 : T + 1],
+                    op0=ALU.mult,
+                    op1=ALU.add,
+                )
+
+        def regroup(dst, planes, on_vector):
+            copy(
+                on_vector,
+                dst.rearrange("p (c i) t -> p c t i", i=4),
+                planes.rearrange("p t (c i) -> p c t i", i=4),
+            )
+
+        def regroup_mix(f, mix, on_vector):
+            mixed[f, mix] = front.tile([P, T, PACK], BF16, tag="mixed", name="mixed", align_bytes=64)
+            regroup(mixed[f, mix][:], mixed_planes[f, mix][:], on_vector)
+
+        def quantise_mix(f, mix):
+            codes = front.tile([P, T], U32, tag="codes%d" % mix, align_bytes=64)
+            plane = front.tile([P, T], U8, tag="plane%d" % mix, align_bytes=64)
+            nc.vector.quantize_mx(
+                out=codes[:].bitcast(FP8X4),
+                scales=plane[:],
+                in_=mixed[f, mix][:].rearrange("p k t -> p (k t)"),
+            )
+            mixes[f, mix] = (codes, plane)
+
+        acc, chi, logit, s, r, sv, state_share, wkv = {}, {}, {}, {}, {}, {}, {}, {}
+
+        def stage1(n, which, bufs):
+            b, j = divmod(n, CH_TILES)
+            codes, plane = mixes[b, which]
+            acc[n, which] = psum.tile([P, T], F32, tag="acc%d" % which, name="acc", bufs=bufs)
             nc.tensor.matmul_mx(
-                out=acc[:],
+                out=acc[n, which][:],
                 lhsT=w_codes[:, which, PACK * P * j : PACK * P * (j + 1)].bitcast(FP8X4),
                 lhsT_scale=w_planes[:, which, P * j : P * (j + 1)],
                 rhs=codes[:].bitcast(FP8X4),
@@ -209,77 +250,167 @@ def tile_rwkv_timemix_pa_t_kernel(
                 start=True,
                 stop=True,
             )
-            return acc
 
-        for b in range(B):
-            mixes = mixes_next
-            if b + 1 < B:
-                mixes_next = mix_and_quantise(b + 1, load_x(b + 1))
+        def gates_without_k(n):
+            b, j = divmod(n, CH_TILES)
+            chi[n] = back.tile([P, T], F32, tag="chi", name="chi")
+            nc.scalar.activation(
+                out=chi[n][:],
+                in_=w_steps[:, j, :],
+                func=ACT.Sigmoid,
+                scale=-1.0,
+                bias=chi_bias[:, j, b : b + 1],
+            )
+            r[n] = back.tile([P, T], F32, tag="r", name="r")
+            nc.scalar.activation(out=r[n][:], in_=acc[n, W_R][:], func=ACT.Sigmoid)
 
-            for j in range(CH_TILES):
-                k_acc = stage1(mixes, W_K, j, "k", 2)
-                v_acc = stage1(mixes, W_V, j, "v", 2)
-                r_acc = stage1(mixes, W_R, j, "r", 1)
+        def make_logit(n):
+            b, j = divmod(n, CH_TILES)
+            logit[n] = back.tile([P, T], F32, tag="logit", name="logit")
+            nc.vector.tensor_sub(out=logit[n][:], in0=acc[n, W_K][:], in1=ln_beta[:, b, j, :])
 
-                chi = back.tile([P, T], F32, tag="chi", bufs=3)
-                nc.scalar.activation(
-                    out=chi[:],
-                    in_=w_steps[:, j, :],
-                    func=ACT.Sigmoid,
-                    scale=-1.0,
-                    bias=chi_bias[:, j, b : b + 1],
-                )
-                logit = back.tile([P, T], F32, tag="logit", bufs=3)
-                nc.vector.tensor_sub(out=logit[:], in0=k_acc[:], in1=ln_beta[:, b, j, :])
-                s = back.tile([P, T], F32, tag="s", bufs=3)
-                nc.scalar.activation(
-                    out=s[:], in_=logit[:], func=ACT.Sigmoid, bias=by_tile[:, j, ROW_U : ROW_U + 1]
-                )
-                r = back.tile([P, T], F32, tag="r", bufs=3)
-                nc.scalar.activation(out=r[:], in_=r_acc[:], func=ACT.Sigmoid)
-
-                state_share = back.tile([P, T], F32, tag="state_share")
-                nc.vector.scalar_tensor_tensor(
-                    out=state_share[:], in0=s[:], scalar=-1.0, in1=chi[:], op0=ALU.add, op1=ALU.mult
-                )
-                sv = back.tile([P, T], F32, tag="sv")
-                nc.vector.tensor_mul(out=sv[:], in0=s[:], in1=v_acc[:])
-                wkv = back.tile([P, T], F32, tag="wkv")
-                nc.vector.scalar_tensor_tensor(
-                    out=wkv[:],
-                    in0=state_share[:],
-                    scalar=neg_alpha[:, j, b : b + 1],
-                    in1=sv[:],
-                    op0=ALU.mult,
-                    op1=ALU.add,
-                )
-                h = back.tile([P, T], F32, tag="h")
-                nc.vector.tensor_mul(out=h[:], in0=wkv[:], in1=r[:])
-                nc.sync.dma_start(out=out[b, P * j : P * (j + 1), :], in_=h[:])
-
-            h_planes = back.tile([P, PACK, T], F32, tag="h_planes")
-            nc.sync.dma_start(out=h_planes[:], in_=out[b].rearrange("(p t) k -> p t k", t=PACK))
-            h_words = back.tile([P, T, PACK], BF16, tag="h_words", align_bytes=64)
-            regroup(h_words[:], h_planes[:])
-            h_codes = back.tile([P, T], U32, tag="h_codes", align_bytes=64)
-            h_plane = back.tile([P, T], U8, tag="h_plane", align_bytes=64)
-            nc.vector.quantize_mx(
-                out=h_codes[:].bitcast(FP8X4),
-                scales=h_plane[:],
-                in_=h_words[:].rearrange("p k t -> p (k t)"),
+        def gate_s(n):
+            j = n % CH_TILES
+            s[n] = back.tile([P, T], F32, tag="s", name="s")
+            nc.scalar.activation(
+                out=s[n][:], in_=logit[n][:], func=ACT.Sigmoid, bias=by_tile[:, j, ROW_U : ROW_U + 1]
             )
 
-            for i in range(TOK_TILES):
-                o_acc = psum.tile([P, C], F32, tag="o", bufs=2)
-                nc.tensor.matmul_mx(
-                    out=o_acc[:],
-                    lhsT=h_codes[:, P * i : P * (i + 1)].bitcast(FP8X4),
-                    lhsT_scale=h_plane[:, P * i : P * (i + 1)],
-                    rhs=w_codes[:, W_OUT, :].bitcast(FP8X4),
-                    rhs_scale=w_planes[:, W_OUT, :],
-                    start=True,
-                    stop=True,
-                )
-                o_sb = back.tile([P, C], F32, tag="o_sb", bufs=4)
-                nc.scalar.copy(out=o_sb[:], in_=o_acc[:])
-                nc.sync.dma_start(out=out[b, P * i : P * (i + 1), :], in_=o_sb[:])
+        def shares(n):
+            sv[n] = back.tile([P, T], F32, tag="sv", name="sv")
+            nc.vector.tensor_mul(out=sv[n][:], in0=s[n][:], in1=acc[n, W_V][:])
+            state_share[n] = back.tile([P, T], F32, tag="state_share", name="state_share")
+            nc.vector.scalar_tensor_tensor(
+                out=state_share[n][:], in0=s[n][:], scalar=-1.0, in1=chi[n][:], op0=ALU.add, op1=ALU.mult
+            )
+
+        def make_wkv(n):
+            b, j = divmod(n, CH_TILES)
+            wkv[n] = back.tile([P, T], F32, tag="wkv", name="wkv")
+            nc.vector.scalar_tensor_tensor(
+                out=wkv[n][:],
+                in0=state_share[n][:],
+                scalar=neg_alpha[:, j, b : b + 1],
+                in1=sv[n][:],
+                op0=ALU.mult,
+                op1=ALU.add,
+            )
+
+        def park_h(n):
+            b, j = divmod(n, CH_TILES)
+            h = back.tile([P, T], F32, tag="h")
+            nc.vector.tensor_mul(out=h[:], in0=wkv[n][:], in1=r[n][:])
+            nc.sync.dma_start(out=out[b, P * j : P * (j + 1), :], in_=h[:])
+
+        h_planes, h_words, h_mx = {}, {}, {}
+
+        def read_back(g):
+            h_planes[g] = back.tile([P, PACK, T], F32, tag="h_planes", name="h_planes")
+            nc.sync.dma_start(out=h_planes[g][:], in_=out[g].rearrange("(p t) k -> p t k", t=PACK))
+
+        def regroup_h(g, on_vector):
+            h_words[g] = back.tile([P, T, PACK], BF16, tag="h_words", name="h_words", align_bytes=64)
+            regroup(h_words[g][:], h_planes[g][:], on_vector)
+
+        def quantise_h(g):
+            codes = back.tile([P, T], U32, tag="h_codes", align_bytes=64)
+            plane = back.tile([P, T], U8, tag="h_plane", align_bytes=64)
+            nc.vector.quantize_mx(
+                out=codes[:].bitcast(FP8X4),
+                scales=plane[:],
+                in_=h_words[g][:].rearrange("p k t -> p (k t)"),
+            )
+            h_mx[g] = (codes, plane)
+
+        def project(g, i, on_vector):
+            codes, plane = h_mx[g]
+            o_acc = psum.tile([P, C], F32, tag="o", bufs=2)
+            nc.tensor.matmul_mx(
+                out=o_acc[:],
+                lhsT=codes[:, P * i : P * (i + 1)].bitcast(FP8X4),
+                lhsT_scale=plane[:, P * i : P * (i + 1)],
+                rhs=w_codes[:, W_OUT, :].bitcast(FP8X4),
+                rhs_scale=w_planes[:, W_OUT, :],
+                start=True,
+                stop=True,
+            )
+            o_sb = back.tile([P, C], F32, tag="o_sb")
+            copy(on_vector, o_sb[:], o_acc[:])
+            nc.sync.dma_start(out=out[g, P * i : P * (i + 1), :], in_=o_sb[:])
+
+        def is_sequence(q):
+            return 0 <= q < B
+
+        def is_unit(n):
+            return 0 <= n < UNITS
+
+        for n in range(FIRST_STEP, LAST_STEP):
+            b, j = divmod(n, CH_TILES)
+            warming_up = n < 0
+            cooling_down = n >= UNITS
+
+            if j == 0 and is_sequence(b - 1):
+                read_back(b - 1)
+            if j == 3 and is_sequence(b + 4):
+                load_x(b + 4)
+            if j == 3 and is_sequence(b - 1):
+                quantise_h(b - 1)
+
+            if is_unit(n + 1):
+                stage1(n + 1, W_K, 1)
+                stage1(n + 1, W_R, 1)
+                gates_without_k(n + 1)
+            if is_unit(n):
+                shares(n)
+            if is_unit(n + 1):
+                stage1(n + 1, W_V, 1)
+                make_logit(n + 1)
+            if is_unit(n):
+                make_wkv(n)
+
+            if is_sequence(n - LN_FIRST_STEP):
+                make_ln_beta(n - LN_FIRST_STEP)
+
+            if j == 0:
+                if is_sequence(b + 1):
+                    quantise_mix(b + 1, W_K)
+                    regroup_mix(b + 1, W_V, warming_up)
+                if is_sequence(b + 2):
+                    mix_plane(b + 2, 1)
+                    difference_plane(b + 2, 2)
+                if is_sequence(b - 2):
+                    project(b - 2, 2, False)
+                    project(b - 2, 3, cooling_down)
+            if j == 1:
+                if is_sequence(b + 1):
+                    quantise_mix(b + 1, W_V)
+                    regroup_mix(b + 1, W_R, warming_up)
+                if is_sequence(b + 2):
+                    mix_plane(b + 2, 2)
+                    difference_plane(b + 2, 3)
+                if is_sequence(b + 3):
+                    transpose_x(b + 3, 0, warming_up)
+            if j == 2:
+                if is_sequence(b + 1):
+                    quantise_mix(b + 1, W_R)
+                if is_sequence(b + 2):
+                    mix_plane(b + 2, 3)
+                if is_sequence(b - 1):
+                    regroup_h(b - 1, cooling_down)
+                if is_sequence(b + 3):
+                    transpose_x(b + 3, 1, warming_up)
+                    difference_plane(b + 3, 0)
+            if j == 3:
+                if is_sequence(b + 3):
+                    mix_plane(b + 3, 0)
+                    difference_plane(b + 3, 1)
+                if is_sequence(b + 2):
+                    regroup_mix(b + 2, W_K, warming_up)
+                if is_sequence(b - 1):
+                    project(b - 1, 0, False)
+                    project(b - 1, 1, cooling_down)
+
+            if is_unit(n + 1):
+                gate_s(n + 1)
+            if is_unit(n):
+                park_h(n)

@@ -117,9 +117,9 @@ def tile_rwkv_timemix_pa_t_kernel(
         a0_col = by_tile[:, :, ROW_A0 : ROW_A0 + B]
         b0_col = by_tile[:, :, ROW_B0 : ROW_B0 + B]
 
-        counts_i32 = back.tile([P, T], I32, tag="o_sb")
+        counts_i32 = back.tile([P, T], I32, tag="o_sb", bufs=3)
         nc.gpsimd.iota(counts_i32[:], pattern=[[1, T]], base=1, channel_multiplier=0)
-        counts = back.tile([P, T], F32, tag="o_sb")
+        counts = back.tile([P, T], F32, tag="o_sb", bufs=3)
         nc.vector.tensor_copy(out=counts[:], in_=counts_i32[:])
         w_steps = const.tile([P, CH_TILES, T], F32)
         for j in range(CH_TILES):
@@ -298,8 +298,8 @@ def tile_rwkv_timemix_pa_t_kernel(
 
         def park_h(n):
             b, j = divmod(n, CH_TILES)
-            h = back.tile([P, T], F32, tag="h")
-            nc.vector.tensor_mul(out=h[:], in0=wkv[n][:], in1=r[n][:])
+            h = back.tile([P, T], F32, tag="h", bufs=3)
+            nc.gpsimd.tensor_mul(out=h[:], in0=wkv[n][:], in1=r[n][:])
             nc.sync.dma_start(out=out[b, P * j : P * (j + 1), :], in_=h[:])
 
         h_planes, h_words, h_mx = {}, {}, {}
@@ -322,7 +322,7 @@ def tile_rwkv_timemix_pa_t_kernel(
             )
             h_mx[g] = (codes, plane)
 
-        def project(g, i, on_vector):
+        def project(g, i):
             codes, plane = h_mx[g]
             o_acc = psum.tile([P, C], F32, tag="o", bufs=2)
             nc.tensor.matmul_mx(
@@ -334,8 +334,8 @@ def tile_rwkv_timemix_pa_t_kernel(
                 start=True,
                 stop=True,
             )
-            o_sb = back.tile([P, C], F32, tag="o_sb")
-            copy(on_vector, o_sb[:], o_acc[:])
+            o_sb = back.tile([P, C], F32, tag="o_sb", bufs=3)
+            copy(i % 2 == 1, o_sb[:], o_acc[:])
             nc.sync.dma_start(out=out[g, P * i : P * (i + 1), :], in_=o_sb[:])
 
         def is_sequence(q):
@@ -353,37 +353,40 @@ def tile_rwkv_timemix_pa_t_kernel(
                 read_back(b - 1)
             if j == 3 and is_sequence(b + 4):
                 load_x(b + 4)
-            if j == 3 and is_sequence(b - 1):
-                quantise_h(b - 1)
 
             if is_unit(n + 1):
                 stage1(n + 1, W_K, 1)
                 stage1(n + 1, W_R, 1)
+                make_logit(n + 1)
                 gates_without_k(n + 1)
+                gate_s(n + 1)
             if is_unit(n):
                 shares(n)
             if is_unit(n + 1):
                 stage1(n + 1, W_V, 1)
-                make_logit(n + 1)
+
+            if j < 3 and is_sequence(b + 1):
+                quantise_mix(b + 1, (W_K, W_V, W_R)[j])
+            if j == 3 and is_sequence(b - 1):
+                quantise_h(b - 1)
             if is_unit(n):
                 make_wkv(n)
+                park_h(n)
 
             if is_sequence(n - LN_FIRST_STEP):
                 make_ln_beta(n - LN_FIRST_STEP)
 
             if j == 0:
                 if is_sequence(b + 1):
-                    quantise_mix(b + 1, W_K)
                     regroup_mix(b + 1, W_V, warming_up)
                 if is_sequence(b + 2):
                     mix_plane(b + 2, 1)
                     difference_plane(b + 2, 2)
                 if is_sequence(b - 2):
-                    project(b - 2, 2, False)
-                    project(b - 2, 3, cooling_down)
+                    project(b - 2, 2)
+                    project(b - 2, 3)
             if j == 1:
                 if is_sequence(b + 1):
-                    quantise_mix(b + 1, W_V)
                     regroup_mix(b + 1, W_R, warming_up)
                 if is_sequence(b + 2):
                     mix_plane(b + 2, 2)
@@ -391,8 +394,6 @@ def tile_rwkv_timemix_pa_t_kernel(
                 if is_sequence(b + 3):
                     transpose_x(b + 3, 0, warming_up)
             if j == 2:
-                if is_sequence(b + 1):
-                    quantise_mix(b + 1, W_R)
                 if is_sequence(b + 2):
                     mix_plane(b + 2, 3)
                 if is_sequence(b - 1):
@@ -407,10 +408,5 @@ def tile_rwkv_timemix_pa_t_kernel(
                 if is_sequence(b + 2):
                     regroup_mix(b + 2, W_K, warming_up)
                 if is_sequence(b - 1):
-                    project(b - 1, 0, False)
-                    project(b - 1, 1, cooling_down)
-
-            if is_unit(n + 1):
-                gate_s(n + 1)
-            if is_unit(n):
-                park_h(n)
+                    project(b - 1, 0)
+                    project(b - 1, 1)

@@ -33,9 +33,21 @@ ROWS = 32
 W_R, W_K, W_V, W_OUT = 0, 1, 2, 3
 
 UNITS = B * CH_TILES
-FIRST_STEP = -13
-LAST_STEP = UNITS + 5
-LN_FIRST_STEP = -B - 1
+MIX_ORDER = (W_K, W_V, W_R)
+
+LOAD_LEAD = 13
+TRANSPOSE_LEAD = 11
+DIFFERENCE_LEAD = 10
+MIX_LEAD = 9
+REGROUP_LEAD = 5
+QUANTISE_LEAD = 4
+LN_BETA_LEAD = B + 1
+READ_BACK_LAG = 4
+REGROUP_H_LAG = 6
+QUANTISE_H_LAG = 10
+PROJECT_LAG = 10
+FIRST_STEP = -TRANSPOSE_LEAD
+LAST_STEP = UNITS - CH_TILES + PROJECT_LAG + 2
 
 
 def tile_rwkv_timemix_pa_t_kernel(
@@ -67,6 +79,14 @@ def tile_rwkv_timemix_pa_t_kernel(
         psum = stack.enter_context(tc.psum_pool(name="psum", bufs=1))
 
         stack.enter_context(tc.manual_schedule())
+
+        x_rows = {}
+
+        def load_x(f):
+            x_rows[f] = front.tile([P, TOK_TILES, C], BF16, tag="x_rows", name="x_rows")
+            nc.sync.dma_start(out=x_rows[f][:], in_=x[f].rearrange("(i p) c -> p i c", p=P))
+
+        load_x(0)
 
         rows = const.tile([P, C], BF16)
         nc.vector.memset(rows[:], 0.0)
@@ -151,17 +171,13 @@ def tile_rwkv_timemix_pa_t_kernel(
                     bias=eps_col[:],
                 )
 
-        x_rows, x_planes, steps, mixed_planes, mixed, mixes = {}, {}, {}, {}, {}, {}
+        x_planes, steps, mixed_planes, mixed, mixes = {}, {}, {}, {}, {}
 
         def copy(on_vector, dst, src):
             if on_vector:
                 nc.vector.tensor_copy(out=dst, in_=src)
             else:
                 nc.scalar.copy(out=dst, in_=src)
-
-        def load_x(f):
-            x_rows[f] = front.tile([P, TOK_TILES, C], BF16, tag="x_rows", name="x_rows")
-            nc.sync.dma_start(out=x_rows[f][:], in_=x[f].rearrange("(i p) c -> p i c", p=P))
 
         def transpose_x(f, pair, on_vector):
             if pair == 0:
@@ -200,7 +216,7 @@ def tile_rwkv_timemix_pa_t_kernel(
                 )
 
         def mix_plane(f, t):
-            for mix in (W_K, W_V, W_R):
+            for mix in MIX_ORDER:
                 if t == 0:
                     mixed_planes[f, mix] = front.tile(
                         [P, PACK, T], BF16, tag="mixed_planes%d" % mix, name="mixed_planes"
@@ -237,10 +253,10 @@ def tile_rwkv_timemix_pa_t_kernel(
 
         acc, chi, logit, s, r, sv, state_share, wkv = {}, {}, {}, {}, {}, {}, {}, {}
 
-        def stage1(n, which, bufs):
+        def stage1(n, which):
             b, j = divmod(n, CH_TILES)
             codes, plane = mixes[b, which]
-            acc[n, which] = psum.tile([P, T], F32, tag="acc%d" % which, name="acc", bufs=bufs)
+            acc[n, which] = psum.tile([P, T], F32, tag="acc%d" % which, name="acc")
             nc.tensor.matmul_mx(
                 out=acc[n, which][:],
                 lhsT=w_codes[:, which, PACK * P * j : PACK * P * (j + 1)].bitcast(FP8X4),
@@ -308,9 +324,22 @@ def tile_rwkv_timemix_pa_t_kernel(
             h_planes[g] = back.tile([P, PACK, T], F32, tag="h_planes", name="h_planes")
             nc.sync.dma_start(out=h_planes[g][:], in_=out[g].rearrange("(p t) k -> p t k", t=PACK))
 
-        def regroup_h(g, on_vector):
-            h_words[g] = back.tile([P, T, PACK], BF16, tag="h_words", name="h_words", align_bytes=64)
-            regroup(h_words[g][:], h_planes[g][:], on_vector)
+        def regroup_h(g, part, on_vector):
+            if part == 0:
+                h_words[g] = back.tile([P, T, PACK], BF16, tag="h_words", name="h_words", align_bytes=64)
+            dst = h_words[g][:, P * part : P * (part + 1), :]
+            planes = h_planes[g][:, :, P * part : P * (part + 1)]
+            if on_vector:
+                regroup(dst, planes, True)
+            else:
+                nc.gpsimd.tensor_scalar(
+                    out=dst,
+                    in0=planes.rearrange("p t k -> p k t"),
+                    scalar1=1.0,
+                    scalar2=0.0,
+                    op0=ALU.mult,
+                    op1=ALU.add,
+                )
 
         def quantise_h(g):
             codes = back.tile([P, T], U32, tag="h_codes", align_bytes=64)
@@ -322,7 +351,7 @@ def tile_rwkv_timemix_pa_t_kernel(
             )
             h_mx[g] = (codes, plane)
 
-        def project(g, i):
+        def project(g, i, on_vector):
             codes, plane = h_mx[g]
             o_acc = psum.tile([P, C], F32, tag="o", bufs=2)
             nc.tensor.matmul_mx(
@@ -335,7 +364,7 @@ def tile_rwkv_timemix_pa_t_kernel(
                 stop=True,
             )
             o_sb = back.tile([P, C], F32, tag="o_sb", bufs=3)
-            copy(i % 2 == 1, o_sb[:], o_acc[:])
+            copy(on_vector, o_sb[:], o_acc[:])
             nc.sync.dma_start(out=out[g, P * i : P * (i + 1), :], in_=o_sb[:])
 
         def is_sequence(q):
@@ -345,68 +374,57 @@ def tile_rwkv_timemix_pa_t_kernel(
             return 0 <= n < UNITS
 
         for n in range(FIRST_STEP, LAST_STEP):
-            b, j = divmod(n, CH_TILES)
             warming_up = n < 0
             cooling_down = n >= UNITS
 
-            if j == 0 and is_sequence(b - 1):
-                read_back(b - 1)
-            if j == 3 and is_sequence(b + 4):
-                load_x(b + 4)
+            f, part = divmod(n - READ_BACK_LAG, CH_TILES)
+            if is_sequence(f) and part == 0:
+                read_back(f)
+            f, part = divmod(n + LOAD_LEAD, CH_TILES)
+            if is_sequence(f) and part == 0:
+                load_x(f)
 
             if is_unit(n + 1):
-                stage1(n + 1, W_K, 1)
-                stage1(n + 1, W_R, 1)
+                stage1(n + 1, W_K)
+                stage1(n + 1, W_R)
                 make_logit(n + 1)
                 gates_without_k(n + 1)
                 gate_s(n + 1)
+
+            f, part = divmod(n + TRANSPOSE_LEAD, CH_TILES)
+            if is_sequence(f) and part < 2:
+                transpose_x(f, part, warming_up)
+            f, part = divmod(n + DIFFERENCE_LEAD, CH_TILES)
+            if is_sequence(f):
+                difference_plane(f, part)
+
             if is_unit(n):
                 shares(n)
             if is_unit(n + 1):
-                stage1(n + 1, W_V, 1)
+                stage1(n + 1, W_V)
 
-            if j < 3 and is_sequence(b + 1):
-                quantise_mix(b + 1, (W_K, W_V, W_R)[j])
-            if j == 3 and is_sequence(b - 1):
-                quantise_h(b - 1)
+            f, part = divmod(n + QUANTISE_LEAD, CH_TILES)
+            if is_sequence(f) and part < 3:
+                quantise_mix(f, MIX_ORDER[part])
+            f, part = divmod(n - QUANTISE_H_LAG, CH_TILES)
+            if is_sequence(f) and part == 0:
+                quantise_h(f)
             if is_unit(n):
                 make_wkv(n)
                 park_h(n)
+            f, part = divmod(n - REGROUP_H_LAG, CH_TILES)
+            if is_sequence(f):
+                regroup_h(f, part, cooling_down)
 
-            if is_sequence(n - LN_FIRST_STEP):
-                make_ln_beta(n - LN_FIRST_STEP)
-
-            if j == 0:
-                if is_sequence(b + 1):
-                    regroup_mix(b + 1, W_V, warming_up)
-                if is_sequence(b + 2):
-                    mix_plane(b + 2, 1)
-                    difference_plane(b + 2, 2)
-                if is_sequence(b - 2):
-                    project(b - 2, 2)
-                    project(b - 2, 3)
-            if j == 1:
-                if is_sequence(b + 1):
-                    regroup_mix(b + 1, W_R, warming_up)
-                if is_sequence(b + 2):
-                    mix_plane(b + 2, 2)
-                    difference_plane(b + 2, 3)
-                if is_sequence(b + 3):
-                    transpose_x(b + 3, 0, warming_up)
-            if j == 2:
-                if is_sequence(b + 2):
-                    mix_plane(b + 2, 3)
-                if is_sequence(b - 1):
-                    regroup_h(b - 1, cooling_down)
-                if is_sequence(b + 3):
-                    transpose_x(b + 3, 1, warming_up)
-                    difference_plane(b + 3, 0)
-            if j == 3:
-                if is_sequence(b + 3):
-                    mix_plane(b + 3, 0)
-                    difference_plane(b + 3, 1)
-                if is_sequence(b + 2):
-                    regroup_mix(b + 2, W_K, warming_up)
-                if is_sequence(b - 1):
-                    project(b - 1, 0)
-                    project(b - 1, 1)
+            if is_sequence(n + LN_BETA_LEAD):
+                make_ln_beta(n + LN_BETA_LEAD)
+            f, part = divmod(n + MIX_LEAD, CH_TILES)
+            if is_sequence(f):
+                mix_plane(f, part)
+            f, part = divmod(n + REGROUP_LEAD, CH_TILES)
+            if is_sequence(f) and part < 3:
+                regroup_mix(f, MIX_ORDER[part], warming_up)
+            f, part = divmod(n - PROJECT_LAG, CH_TILES)
+            if is_sequence(f) and part < 2:
+                project(f, 2 * part, False)
+                project(f, 2 * part + 1, cooling_down)

@@ -1,4 +1,3 @@
-import math
 from contextlib import ExitStack
 
 import concourse.mybir as mybir
@@ -44,8 +43,8 @@ QUANTISE_LEAD = 4
 LN_BETA_LEAD = B + 1
 READ_BACK_LAG = 4
 REGROUP_H_LAG = 6
-QUANTISE_H_LAG = 10
-PROJECT_LAG = 10
+QUANTISE_H_LAG = 7
+PROJECT_LAG = 7
 FIRST_STEP = -TRANSPOSE_LEAD
 LAST_STEP = UNITS - CH_TILES + PROJECT_LAG + 2
 
@@ -324,22 +323,9 @@ def tile_rwkv_timemix_pa_t_kernel(
             h_planes[g] = back.tile([P, PACK, T], F32, tag="h_planes", name="h_planes")
             nc.sync.dma_start(out=h_planes[g][:], in_=out[g].rearrange("(p t) k -> p t k", t=PACK))
 
-        def regroup_h(g, part, on_vector):
-            if part == 0:
-                h_words[g] = back.tile([P, T, PACK], BF16, tag="h_words", name="h_words", align_bytes=64)
-            dst = h_words[g][:, P * part : P * (part + 1), :]
-            planes = h_planes[g][:, :, P * part : P * (part + 1)]
-            if on_vector:
-                regroup(dst, planes, True)
-            else:
-                nc.gpsimd.tensor_scalar(
-                    out=dst,
-                    in0=planes.rearrange("p t k -> p k t"),
-                    scalar1=1.0,
-                    scalar2=0.0,
-                    op0=ALU.mult,
-                    op1=ALU.add,
-                )
+        def regroup_h(g, on_vector):
+            h_words[g] = back.tile([P, T, PACK], BF16, tag="h_words", name="h_words", align_bytes=64)
+            regroup(h_words[g][:], h_planes[g][:], on_vector)
 
         def quantise_h(g):
             codes = back.tile([P, T], U32, tag="h_codes", align_bytes=64)
@@ -351,7 +337,7 @@ def tile_rwkv_timemix_pa_t_kernel(
             )
             h_mx[g] = (codes, plane)
 
-        def project(g, i, on_vector):
+        def project(g, i):
             codes, plane = h_mx[g]
             o_acc = psum.tile([P, C], F32, tag="o", bufs=2)
             nc.tensor.matmul_mx(
@@ -364,7 +350,7 @@ def tile_rwkv_timemix_pa_t_kernel(
                 stop=True,
             )
             o_sb = back.tile([P, C], F32, tag="o_sb", bufs=3)
-            copy(on_vector, o_sb[:], o_acc[:])
+            copy(i % 2 == 1, o_sb[:], o_acc[:])
             nc.sync.dma_start(out=out[g, P * i : P * (i + 1), :], in_=o_sb[:])
 
         def is_sequence(q):
@@ -412,9 +398,6 @@ def tile_rwkv_timemix_pa_t_kernel(
             if is_unit(n):
                 make_wkv(n)
                 park_h(n)
-            f, part = divmod(n - REGROUP_H_LAG, CH_TILES)
-            if is_sequence(f):
-                regroup_h(f, part, cooling_down)
 
             if is_sequence(n + LN_BETA_LEAD):
                 make_ln_beta(n + LN_BETA_LEAD)
@@ -424,7 +407,10 @@ def tile_rwkv_timemix_pa_t_kernel(
             f, part = divmod(n + REGROUP_LEAD, CH_TILES)
             if is_sequence(f) and part < 3:
                 regroup_mix(f, MIX_ORDER[part], warming_up)
+            f, part = divmod(n - REGROUP_H_LAG, CH_TILES)
+            if is_sequence(f) and part == 0:
+                regroup_h(f, cooling_down)
             f, part = divmod(n - PROJECT_LAG, CH_TILES)
             if is_sequence(f) and part < 2:
-                project(f, 2 * part, False)
-                project(f, 2 * part + 1, cooling_down)
+                project(f, 2 * part)
+                project(f, 2 * part + 1)

@@ -15,7 +15,6 @@ ACT = mybir.ActivationFunctionType
 P = 128
 PACK = 4
 B, T, C = 8, 512, 512
-CH_TILES = C // P
 TOK_TILES = T // P
 EPS = 1e-8
 
@@ -31,7 +30,7 @@ ROWS = 32
 
 W_R, W_K, W_V, W_OUT = 0, 1, 2, 3
 
-UNITS = B * CH_TILES
+UNITS = B * PACK
 MIX_ORDER = (W_K, W_V, W_R)
 
 LOAD_LEAD = 13
@@ -41,12 +40,12 @@ MIX_LEAD = 9
 REGROUP_LEAD = 5
 QUANTISE_LEAD = 4
 LN_BETA_LEAD = B + 1
-READ_BACK_LAG = 4
-REGROUP_H_LAG = 6
-QUANTISE_H_LAG = 7
-PROJECT_LAG = 7
+PERMUTE_STEP = -9
+H_LAG = 4
+QUANTISE_H_LAG = 5
+PROJECT_LAG = 6
 FIRST_STEP = -TRANSPOSE_LEAD
-LAST_STEP = UNITS - CH_TILES + PROJECT_LAG + 2
+LAST_STEP = UNITS - PACK + PROJECT_LAG + TOK_TILES
 
 
 def tile_rwkv_timemix_pa_t_kernel(
@@ -89,15 +88,15 @@ def tile_rwkv_timemix_pa_t_kernel(
 
         rows = const.tile([P, C], BF16)
         nc.vector.memset(rows[:], 0.0)
-        nc.sync.dma_start(out=rows[ROW_A0 : ROW_A0 + B, :], in_=a0)
-        nc.sync.dma_start(out=rows[ROW_B0 : ROW_B0 + B, :], in_=b0)
-        nc.sync.dma_start(out=rows[ROW_XPREV : ROW_XPREV + B, :], in_=x_prev0)
+        nc.scalar.dma_start(out=rows[ROW_A0 : ROW_A0 + B, :], in_=a0)
+        nc.scalar.dma_start(out=rows[ROW_B0 : ROW_B0 + B, :], in_=b0)
+        nc.scalar.dma_start(out=rows[ROW_XPREV : ROW_XPREV + B, :], in_=x_prev0)
         for row, vector in ((ROW_W, w), (ROW_U, u), (ROW_MU, mu_r), (ROW_MU + 1, mu_k), (ROW_MU + 2, mu_v)):
-            nc.sync.dma_start(out=rows[row : row + 1, :], in_=vector.unsqueeze(0))
+            nc.scalar.dma_start(out=rows[row : row + 1, :], in_=vector.unsqueeze(0))
 
-        w_codes = const.tile([P, 4, PACK * C], U8, align_bytes=64)
-        w_planes = const.tile([P, 4, C], U8, align_bytes=64)
-        nc.vector.memset(w_planes[:].rearrange("p w n -> p (w n)").bitcast(I32), 0)
+        arrived_codes = const.tile([P, 4, PACK * C], U8, align_bytes=64)
+        arrived_planes = const.tile([P, 4, C], U8, align_bytes=64)
+        nc.vector.memset(arrived_planes[:].rearrange("p w n -> p (w n)").bitcast(I32), 0)
         weights = (
             (W_r_words, W_r_scales),
             (W_k_words, W_k_scales),
@@ -106,13 +105,27 @@ def tile_rwkv_timemix_pa_t_kernel(
         )
         for wi, (words, scales) in enumerate(weights):
             nc.sync.dma_start(
-                out=w_codes[:, wi, :].bitcast(I32),
+                out=arrived_codes[:, wi, :].bitcast(I32),
                 in_=words[0].rearrange("p n t -> p (n t)").bitcast(I32),
             )
             for quadrant in range(4):
                 nc.sync.dma_start(
-                    out=w_planes[32 * quadrant : 32 * quadrant + 4, wi, :].bitcast(I32),
+                    out=arrived_planes[32 * quadrant : 32 * quadrant + 4, wi, :].bitcast(I32),
                     in_=scales[0, 4 * quadrant : 4 * quadrant + 4, :].bitcast(I32),
+                )
+
+        w_codes = const.tile([P, 3, PACK * C], U8, align_bytes=64)
+        w_planes = const.tile([P, 3, C], U8, align_bytes=64)
+
+        def permute_columns():
+            for wi in (W_K, W_R, W_V):
+                nc.gpsimd.tensor_copy(
+                    out=w_codes[:, wi, :].bitcast(I32).rearrange("p (t m) -> p t m", t=PACK),
+                    in_=arrived_codes[:, wi, :].bitcast(I32).rearrange("p (m t) -> p t m", t=PACK),
+                )
+                nc.gpsimd.tensor_copy(
+                    out=w_planes[:, wi, :].rearrange("p (t m) -> p m t", t=PACK),
+                    in_=arrived_planes[:, wi, :].rearrange("p (m t) -> p m t", t=PACK),
                 )
 
         ident_bf16 = const.tile([P, P], BF16)
@@ -124,49 +137,45 @@ def tile_rwkv_timemix_pa_t_kernel(
         neg_ident = const.tile([P, P], BF16)
         nc.vector.tensor_scalar_mul(out=neg_ident[:], in0=ident_bf16[:], scalar1=-1.0)
 
-        rows_t = psum.tile([P, 2 * CH_TILES, P], BF16, tag="xt")
-        for j in range(CH_TILES):
-            nc.tensor.transpose(rows_t[:, j, :], rows[:, P * j : P * (j + 1)], ident_bf16[:])
+        rows_t = psum.tile([P, PACK, P], BF16, tag="xt")
         for t in range(PACK):
-            nc.tensor.transpose(rows_t[:, CH_TILES + t, :], rows[:, t:C:PACK], ident_bf16[:])
-        cols = const.tile([P, 2 * CH_TILES, ROWS], F32)
+            nc.tensor.transpose(rows_t[:, t, :], rows[:, t:C:PACK], ident_bf16[:])
+        cols = const.tile([P, PACK, ROWS], F32)
         nc.vector.tensor_copy(out=cols[:], in_=rows_t[:, :, 0:ROWS])
-        by_tile = cols[:, 0:CH_TILES, :]
-        by_word = cols[:, CH_TILES : CH_TILES + PACK, :]
-        a0_col = by_tile[:, :, ROW_A0 : ROW_A0 + B]
-        b0_col = by_tile[:, :, ROW_B0 : ROW_B0 + B]
+        a0_col = cols[:, :, ROW_A0 : ROW_A0 + B]
+        b0_col = cols[:, :, ROW_B0 : ROW_B0 + B]
+        negated = const.tile([P, PACK, 2], F32)
+        nc.vector.tensor_scalar_mul(out=negated[:], in0=cols[:, :, ROW_W : ROW_U + 1], scalar1=-1.0)
+        neg_w = negated[:, :, 0]
+        neg_u = negated[:, :, 1]
 
         counts_i32 = back.tile([P, T], I32, tag="o_sb", bufs=3)
         nc.gpsimd.iota(counts_i32[:], pattern=[[1, T]], base=1, channel_multiplier=0)
-        counts = back.tile([P, T], F32, tag="o_sb", bufs=3)
+        counts = const.tile([P, T], F32)
         nc.vector.tensor_copy(out=counts[:], in_=counts_i32[:])
-        w_steps = const.tile([P, CH_TILES, T], F32)
-        for j in range(CH_TILES):
-            nc.vector.tensor_scalar_mul(
-                out=w_steps[:, j, :], in0=counts[:], scalar1=by_tile[:, j, ROW_W : ROW_W + 1]
-            )
-        decay = back.tile([P, CH_TILES, T], F32, tag="h_planes")
-        nc.scalar.activation(out=decay[:], in_=w_steps[:], func=ACT.Exp, scale=-1.0)
-        chi_bias = const.tile([P, CH_TILES, B], F32)
+        decay = back.tile([P, PACK, T], F32, tag="r_planes", bufs=3)
+        for t in range(PACK):
+            nc.scalar.activation(out=decay[:, t, :], in_=counts[:], func=ACT.Exp, scale=neg_w[:, t : t + 1])
+        chi_bias = const.tile([P, PACK, B], F32)
         nc.scalar.activation(out=chi_bias[:], in_=b0_col, func=ACT.Ln, scale=1.0 / EPS)
 
-        neg_alpha = const.tile([P, CH_TILES, B], F32)
-        b0_inverse = const.tile([P, CH_TILES, B], F32)
+        neg_alpha = const.tile([P, PACK, B], F32)
+        b0_inverse = const.tile([P, PACK, B], F32)
         nc.vector.reciprocal(b0_inverse[:], b0_col)
         nc.vector.scalar_tensor_tensor(
             out=neg_alpha[:], in0=a0_col, scalar=-1.0, in1=b0_inverse[:], op0=ALU.mult, op1=ALU.mult
         )
         eps_col = const.tile([P, 1], F32)
         nc.vector.memset(eps_col[:], EPS)
-        ln_beta = const.tile([P, B, CH_TILES, T], F32)
+        ln_beta = const.tile([P, B, PACK, T], F32)
 
         def make_ln_beta(q):
-            for j in range(CH_TILES):
+            for t in range(PACK):
                 nc.scalar.activation(
-                    out=ln_beta[:, q, j, :],
-                    in_=decay[:, j, :],
+                    out=ln_beta[:, q, t, :],
+                    in_=decay[:, t, :],
                     func=ACT.Ln,
-                    scale=b0_col[:, j, q : q + 1],
+                    scale=b0_col[:, t, q : q + 1],
                     bias=eps_col[:],
                 )
 
@@ -181,7 +190,7 @@ def tile_rwkv_timemix_pa_t_kernel(
         def transpose_x(f, pair, on_vector):
             if pair == 0:
                 x_planes[f] = front.tile([P, PACK, T + 2], BF16, tag="x_planes", name="x_planes")
-                copy(on_vector, x_planes[f][:, :, 1], by_word[:, :, ROW_XPREV + f])
+                copy(on_vector, x_planes[f][:, :, 1], cols[:, :, ROW_XPREV + f])
             xt = psum.tile([P, 2, T], BF16, tag="xt")
             for e in range(2):
                 for i in range(TOK_TILES):
@@ -223,22 +232,19 @@ def tile_rwkv_timemix_pa_t_kernel(
                 nc.vector.scalar_tensor_tensor(
                     out=mixed_planes[f, mix][:, t, :],
                     in0=steps[f, t][:],
-                    scalar=by_word[:, t, ROW_MU + mix : ROW_MU + mix + 1],
+                    scalar=cols[:, t, ROW_MU + mix : ROW_MU + mix + 1],
                     in1=x_planes[f][:, t, 1 : T + 1],
                     op0=ALU.mult,
                     op1=ALU.add,
                 )
 
-        def regroup(dst, planes, on_vector):
-            copy(
-                on_vector,
-                dst.rearrange("p (c i) t -> p c t i", i=4),
-                planes.rearrange("p t (c i) -> p c t i", i=4),
-            )
-
         def regroup_mix(f, mix, on_vector):
             mixed[f, mix] = front.tile([P, T, PACK], BF16, tag="mixed", name="mixed", align_bytes=64)
-            regroup(mixed[f, mix][:], mixed_planes[f, mix][:], on_vector)
+            copy(
+                on_vector,
+                mixed[f, mix][:].rearrange("p (c i) t -> p c t i", i=4),
+                mixed_planes[f, mix][:].rearrange("p t (c i) -> p c t i", i=4),
+            )
 
         def quantise_mix(f, mix):
             codes = front.tile([P, T], U32, tag="codes%d" % mix, align_bytes=64)
@@ -250,16 +256,16 @@ def tile_rwkv_timemix_pa_t_kernel(
             )
             mixes[f, mix] = (codes, plane)
 
-        acc, chi, logit, s, r, sv, state_share, wkv = {}, {}, {}, {}, {}, {}, {}, {}
+        acc, chi, logit, ns, r_planes, bracket, ns_bracket, wkv_planes = {}, {}, {}, {}, {}, {}, {}, {}
 
         def stage1(n, which):
-            b, j = divmod(n, CH_TILES)
+            b, t = divmod(n, PACK)
             codes, plane = mixes[b, which]
-            acc[n, which] = psum.tile([P, T], F32, tag="acc%d" % which, name="acc")
+            acc[n, which] = psum.tile([P, T], F32, tag="acc%d" % which, name="acc", bufs=2 if which == W_V else 1)
             nc.tensor.matmul_mx(
                 out=acc[n, which][:],
-                lhsT=w_codes[:, which, PACK * P * j : PACK * P * (j + 1)].bitcast(FP8X4),
-                lhsT_scale=w_planes[:, which, P * j : P * (j + 1)],
+                lhsT=w_codes[:, which, PACK * P * t : PACK * P * (t + 1)].bitcast(FP8X4),
+                lhsT_scale=w_planes[:, which, P * t : P * (t + 1)],
                 rhs=codes[:].bitcast(FP8X4),
                 rhs_scale=plane[:],
                 start=True,
@@ -267,90 +273,86 @@ def tile_rwkv_timemix_pa_t_kernel(
             )
 
         def gates_without_k(n):
-            b, j = divmod(n, CH_TILES)
+            b, t = divmod(n, PACK)
             chi[n] = back.tile([P, T], F32, tag="chi", name="chi")
             nc.scalar.activation(
                 out=chi[n][:],
-                in_=w_steps[:, j, :],
+                in_=counts[:],
                 func=ACT.Sigmoid,
-                scale=-1.0,
-                bias=chi_bias[:, j, b : b + 1],
+                scale=neg_w[:, t : t + 1],
+                bias=chi_bias[:, t, b : b + 1],
             )
-            r[n] = back.tile([P, T], F32, tag="r", name="r")
-            nc.scalar.activation(out=r[n][:], in_=acc[n, W_R][:], func=ACT.Sigmoid)
+            if t == 0:
+                r_planes[b] = back.tile([P, PACK, T], F32, tag="r_planes", name="r_planes", bufs=3)
+            nc.scalar.activation(out=r_planes[b][:, t, :], in_=acc[n, W_R][:], func=ACT.Sigmoid)
 
         def make_logit(n):
-            b, j = divmod(n, CH_TILES)
+            b, t = divmod(n, PACK)
             logit[n] = back.tile([P, T], F32, tag="logit", name="logit")
-            nc.vector.tensor_sub(out=logit[n][:], in0=acc[n, W_K][:], in1=ln_beta[:, b, j, :])
+            nc.vector.tensor_sub(out=logit[n][:], in0=acc[n, W_K][:], in1=ln_beta[:, b, t, :])
 
-        def gate_s(n):
-            j = n % CH_TILES
-            s[n] = back.tile([P, T], F32, tag="s", name="s")
+        def gate_ns(n):
+            t = n % PACK
+            ns[n] = back.tile([P, T], F32, tag="ns", name="ns")
             nc.scalar.activation(
-                out=s[n][:], in_=logit[n][:], func=ACT.Sigmoid, bias=by_tile[:, j, ROW_U : ROW_U + 1]
+                out=ns[n][:], in_=logit[n][:], func=ACT.Sigmoid, scale=-1.0, bias=neg_u[:, t : t + 1]
             )
 
-        def shares(n):
-            sv[n] = back.tile([P, T], F32, tag="sv", name="sv")
-            nc.vector.tensor_mul(out=sv[n][:], in0=s[n][:], in1=acc[n, W_V][:])
-            state_share[n] = back.tile([P, T], F32, tag="state_share", name="state_share")
+        def make_bracket(n):
+            b, t = divmod(n, PACK)
+            bracket[n] = back.tile([P, T], F32, tag="bracket", name="bracket")
             nc.vector.scalar_tensor_tensor(
-                out=state_share[n][:], in0=s[n][:], scalar=-1.0, in1=chi[n][:], op0=ALU.add, op1=ALU.mult
-            )
-
-        def make_wkv(n):
-            b, j = divmod(n, CH_TILES)
-            wkv[n] = back.tile([P, T], F32, tag="wkv", name="wkv")
-            nc.vector.scalar_tensor_tensor(
-                out=wkv[n][:],
-                in0=state_share[n][:],
-                scalar=neg_alpha[:, j, b : b + 1],
-                in1=sv[n][:],
+                out=bracket[n][:],
+                in0=chi[n][:],
+                scalar=neg_alpha[:, t, b : b + 1],
+                in1=acc[n, W_V][:],
                 op0=ALU.mult,
                 op1=ALU.add,
             )
+            ns_bracket[n] = back.tile([P, T], F32, tag="ns_bracket", name="ns_bracket")
+            nc.gpsimd.tensor_mul(out=ns_bracket[n][:], in0=bracket[n][:], in1=ns[n][:])
 
-        def park_h(n):
-            b, j = divmod(n, CH_TILES)
-            h = back.tile([P, T], F32, tag="h", bufs=3)
-            nc.gpsimd.tensor_mul(out=h[:], in0=wkv[n][:], in1=r[n][:])
-            nc.sync.dma_start(out=out[b, P * j : P * (j + 1), :], in_=h[:])
+        def make_wkv(n):
+            b, t = divmod(n, PACK)
+            if t == 0:
+                wkv_planes[b] = back.tile([P, PACK, T], F32, tag="wkv_planes", name="wkv_planes")
+            nc.vector.tensor_sub(out=wkv_planes[b][:, t, :], in0=acc[n, W_V][:], in1=ns_bracket[n][:])
 
-        h_planes, h_words, h_mx = {}, {}, {}
+        h_words, h_mx = {}, {}
 
-        def read_back(g):
-            h_planes[g] = back.tile([P, PACK, T], F32, tag="h_planes", name="h_planes")
-            nc.sync.dma_start(out=h_planes[g][:], in_=out[g].rearrange("(p t) k -> p t k", t=PACK))
+        def make_h(g, i, on_vector):
+            h_words[g, i] = back.tile([P, P, PACK], BF16, tag="h_words", name="h_words", bufs=3, align_bytes=64)
+            engine = nc.vector if on_vector else nc.gpsimd
+            engine.tensor_mul(
+                out=h_words[g, i][:],
+                in0=wkv_planes[g][:, :, P * i : P * (i + 1)].rearrange("p t k -> p k t"),
+                in1=r_planes[g][:, :, P * i : P * (i + 1)].rearrange("p t k -> p k t"),
+            )
 
-        def regroup_h(g, on_vector):
-            h_words[g] = back.tile([P, T, PACK], BF16, tag="h_words", name="h_words", align_bytes=64)
-            regroup(h_words[g][:], h_planes[g][:], on_vector)
-
-        def quantise_h(g):
-            codes = back.tile([P, T], U32, tag="h_codes", align_bytes=64)
-            plane = back.tile([P, T], U8, tag="h_plane", align_bytes=64)
+        def quantise_h(g, i):
+            codes = back.tile([P, P], U32, tag="h_codes", bufs=3, align_bytes=64)
+            plane = back.tile([P, P], U8, tag="h_plane", bufs=3, align_bytes=64)
             nc.vector.quantize_mx(
                 out=codes[:].bitcast(FP8X4),
                 scales=plane[:],
-                in_=h_words[g][:].rearrange("p k t -> p (k t)"),
+                in_=h_words[g, i][:].rearrange("p k t -> p (k t)"),
             )
-            h_mx[g] = (codes, plane)
+            h_mx[g, i] = (codes, plane)
 
-        def project(g, i):
-            codes, plane = h_mx[g]
-            o_acc = psum.tile([P, C], F32, tag="o", bufs=2)
+        def project(g, i, on_vector):
+            codes, plane = h_mx[g, i]
+            o_acc = psum.tile([P, C], F32, tag="o")
             nc.tensor.matmul_mx(
                 out=o_acc[:],
-                lhsT=codes[:, P * i : P * (i + 1)].bitcast(FP8X4),
-                lhsT_scale=plane[:, P * i : P * (i + 1)],
-                rhs=w_codes[:, W_OUT, :].bitcast(FP8X4),
-                rhs_scale=w_planes[:, W_OUT, :],
+                lhsT=codes[:].bitcast(FP8X4),
+                lhsT_scale=plane[:],
+                rhs=arrived_codes[:, W_OUT, :].bitcast(FP8X4),
+                rhs_scale=arrived_planes[:, W_OUT, :],
                 start=True,
                 stop=True,
             )
             o_sb = back.tile([P, C], F32, tag="o_sb", bufs=3)
-            copy(i % 2 == 1, o_sb[:], o_acc[:])
+            copy(on_vector, o_sb[:], o_acc[:])
             nc.sync.dma_start(out=out[g, P * i : P * (i + 1), :], in_=o_sb[:])
 
         def is_sequence(q):
@@ -363,54 +365,51 @@ def tile_rwkv_timemix_pa_t_kernel(
             warming_up = n < 0
             cooling_down = n >= UNITS
 
-            f, part = divmod(n - READ_BACK_LAG, CH_TILES)
-            if is_sequence(f) and part == 0:
-                read_back(f)
-            f, part = divmod(n + LOAD_LEAD, CH_TILES)
+            f, part = divmod(n + LOAD_LEAD, PACK)
             if is_sequence(f) and part == 0:
                 load_x(f)
+            if n == PERMUTE_STEP:
+                permute_columns()
 
+            f, part = divmod(n - PROJECT_LAG, TOK_TILES)
+            if is_sequence(f):
+                project(f, part, cooling_down and part % 2 == 1)
             if is_unit(n + 1):
                 stage1(n + 1, W_K)
                 stage1(n + 1, W_R)
-                make_logit(n + 1)
+                stage1(n + 1, W_V)
+            if is_unit(n):
+                make_bracket(n)
+            if is_unit(n + 1):
                 gates_without_k(n + 1)
-                gate_s(n + 1)
 
-            f, part = divmod(n + TRANSPOSE_LEAD, CH_TILES)
+            f, part = divmod(n + TRANSPOSE_LEAD, PACK)
             if is_sequence(f) and part < 2:
                 transpose_x(f, part, warming_up)
-            f, part = divmod(n + DIFFERENCE_LEAD, CH_TILES)
+            f, part = divmod(n + DIFFERENCE_LEAD, PACK)
             if is_sequence(f):
                 difference_plane(f, part)
-
-            if is_unit(n):
-                shares(n)
-            if is_unit(n + 1):
-                stage1(n + 1, W_V)
-
-            f, part = divmod(n + QUANTISE_LEAD, CH_TILES)
-            if is_sequence(f) and part < 3:
-                quantise_mix(f, MIX_ORDER[part])
-            f, part = divmod(n - QUANTISE_H_LAG, CH_TILES)
-            if is_sequence(f) and part == 0:
-                quantise_h(f)
-            if is_unit(n):
-                make_wkv(n)
-                park_h(n)
-
-            if is_sequence(n + LN_BETA_LEAD):
-                make_ln_beta(n + LN_BETA_LEAD)
-            f, part = divmod(n + MIX_LEAD, CH_TILES)
+            f, part = divmod(n + MIX_LEAD, PACK)
             if is_sequence(f):
                 mix_plane(f, part)
-            f, part = divmod(n + REGROUP_LEAD, CH_TILES)
+            f, part = divmod(n + REGROUP_LEAD, PACK)
             if is_sequence(f) and part < 3:
                 regroup_mix(f, MIX_ORDER[part], warming_up)
-            f, part = divmod(n - REGROUP_H_LAG, CH_TILES)
-            if is_sequence(f) and part == 0:
-                regroup_h(f, cooling_down)
-            f, part = divmod(n - PROJECT_LAG, CH_TILES)
-            if is_sequence(f) and part < 2:
-                project(f, 2 * part)
-                project(f, 2 * part + 1)
+
+            if is_unit(n + 1):
+                make_logit(n + 1)
+                gate_ns(n + 1)
+            f, part = divmod(n - H_LAG, TOK_TILES)
+            if is_sequence(f):
+                make_h(f, part, cooling_down)
+            if is_unit(n):
+                make_wkv(n)
+
+            f, part = divmod(n + QUANTISE_LEAD, PACK)
+            if is_sequence(f) and part < 3:
+                quantise_mix(f, MIX_ORDER[part])
+            f, part = divmod(n - QUANTISE_H_LAG, TOK_TILES)
+            if is_sequence(f):
+                quantise_h(f, part)
+            if is_sequence(n + LN_BETA_LEAD):
+                make_ln_beta(n + LN_BETA_LEAD)

@@ -43,7 +43,7 @@ LN_BETA_LEAD = B + 1
 PERMUTE_STEP = -9
 H_LAG = 4
 QUANTISE_H_LAG = 5
-PROJECT_LAG = 6
+PROJECT_LAG = 5
 FIRST_STEP = -TRANSPOSE_LEAD
 LAST_STEP = UNITS - PACK + PROJECT_LAG + TOK_TILES
 
@@ -88,11 +88,17 @@ def tile_rwkv_timemix_pa_t_kernel(
 
         rows = const.tile([P, C], BF16)
         nc.vector.memset(rows[:], 0.0)
-        nc.scalar.dma_start(out=rows[ROW_A0 : ROW_A0 + B, :], in_=a0)
-        nc.scalar.dma_start(out=rows[ROW_B0 : ROW_B0 + B, :], in_=b0)
+        nc.sync.dma_start(out=rows[ROW_B0 : ROW_B0 + B, :], in_=b0)
         nc.scalar.dma_start(out=rows[ROW_XPREV : ROW_XPREV + B, :], in_=x_prev0)
-        for row, vector in ((ROW_W, w), (ROW_U, u), (ROW_MU, mu_r), (ROW_MU + 1, mu_k), (ROW_MU + 2, mu_v)):
-            nc.scalar.dma_start(out=rows[row : row + 1, :], in_=vector.unsqueeze(0))
+        nc.sync.dma_start(out=rows[ROW_A0 : ROW_A0 + B, :], in_=a0)
+        for queue, row, vector in (
+            (nc.sync, ROW_W, w),
+            (nc.scalar, ROW_MU, mu_r),
+            (nc.sync, ROW_U, u),
+            (nc.scalar, ROW_MU + 1, mu_k),
+            (nc.scalar, ROW_MU + 2, mu_v),
+        ):
+            queue.dma_start(out=rows[row : row + 1, :], in_=vector.unsqueeze(0))
 
         arrived_codes = const.tile([P, 4, PACK * C], U8, align_bytes=64)
         arrived_planes = const.tile([P, 4, C], U8, align_bytes=64)
@@ -137,37 +143,38 @@ def tile_rwkv_timemix_pa_t_kernel(
         neg_ident = const.tile([P, P], BF16)
         nc.vector.tensor_scalar_mul(out=neg_ident[:], in0=ident_bf16[:], scalar1=-1.0)
 
-        rows_t = psum.tile([P, PACK, P], BF16, tag="xt")
-        for t in range(PACK):
-            nc.tensor.transpose(rows_t[:, t, :], rows[:, t:C:PACK], ident_bf16[:])
-        cols = const.tile([P, PACK, ROWS], F32)
-        nc.vector.tensor_copy(out=cols[:], in_=rows_t[:, :, 0:ROWS])
-        a0_col = cols[:, :, ROW_A0 : ROW_A0 + B]
-        b0_col = cols[:, :, ROW_B0 : ROW_B0 + B]
-        negated = const.tile([P, PACK, 2], F32)
-        nc.vector.tensor_scalar_mul(out=negated[:], in0=cols[:, :, ROW_W : ROW_U + 1], scalar1=-1.0)
-        neg_w = negated[:, :, 0]
-        neg_u = negated[:, :, 1]
-
         counts_i32 = back.tile([P, T], I32, tag="o_sb", bufs=3)
         nc.gpsimd.iota(counts_i32[:], pattern=[[1, T]], base=1, channel_multiplier=0)
         counts = const.tile([P, T], F32)
         nc.vector.tensor_copy(out=counts[:], in_=counts_i32[:])
-        decay = back.tile([P, PACK, T], F32, tag="r_planes", bufs=3)
-        for t in range(PACK):
-            nc.scalar.activation(out=decay[:, t, :], in_=counts[:], func=ACT.Exp, scale=neg_w[:, t : t + 1])
-        chi_bias = const.tile([P, PACK, B], F32)
-        nc.scalar.activation(out=chi_bias[:], in_=b0_col, func=ACT.Ln, scale=1.0 / EPS)
-
-        neg_alpha = const.tile([P, PACK, B], F32)
-        b0_inverse = const.tile([P, PACK, B], F32)
-        nc.vector.reciprocal(b0_inverse[:], b0_col)
-        nc.vector.scalar_tensor_tensor(
-            out=neg_alpha[:], in0=a0_col, scalar=-1.0, in1=b0_inverse[:], op0=ALU.mult, op1=ALU.mult
-        )
         eps_col = const.tile([P, 1], F32)
         nc.vector.memset(eps_col[:], EPS)
+
+        cols = const.tile([P, PACK, ROWS], F32)
+        a0_col = cols[:, :, ROW_A0 : ROW_A0 + B]
+        b0_col = cols[:, :, ROW_B0 : ROW_B0 + B]
+        negated = const.tile([P, PACK, 2], F32)
+        neg_w = negated[:, :, 0]
+        neg_u = negated[:, :, 1]
+        chi_bias = const.tile([P, PACK, B], F32)
+        neg_alpha = const.tile([P, PACK, B], F32)
+        b0_inverse = const.tile([P, PACK, B], F32)
         ln_beta = const.tile([P, B, PACK, T], F32)
+        decay = back.tile([P, PACK, T], F32, tag="r_planes", bufs=3)
+
+        def per_channel_numbers():
+            rows_t = psum.tile([P, PACK, P], BF16, tag="o")
+            for t in range(PACK):
+                nc.tensor.transpose(rows_t[:, t, :], rows[:, t:C:PACK], ident_bf16[:])
+            nc.vector.tensor_copy(out=cols[:], in_=rows_t[:, :, 0:ROWS])
+            nc.vector.tensor_scalar_mul(out=negated[:], in0=cols[:, :, ROW_W : ROW_U + 1], scalar1=-1.0)
+            for t in range(PACK):
+                nc.scalar.activation(out=decay[:, t, :], in_=counts[:], func=ACT.Exp, scale=neg_w[:, t : t + 1])
+            nc.scalar.activation(out=chi_bias[:], in_=b0_col, func=ACT.Ln, scale=1.0 / EPS)
+            nc.vector.reciprocal(b0_inverse[:], b0_col)
+            nc.vector.scalar_tensor_tensor(
+                out=neg_alpha[:], in0=a0_col, scalar=-1.0, in1=b0_inverse[:], op0=ALU.mult, op1=ALU.mult
+            )
 
         def make_ln_beta(q):
             for t in range(PACK):
@@ -190,6 +197,7 @@ def tile_rwkv_timemix_pa_t_kernel(
         def transpose_x(f, pair, on_vector):
             if pair == 0:
                 x_planes[f] = front.tile([P, PACK, T + 2], BF16, tag="x_planes", name="x_planes")
+            else:
                 copy(on_vector, x_planes[f][:, :, 1], cols[:, :, ROW_XPREV + f])
             xt = psum.tile([P, 2, T], BF16, tag="xt")
             for e in range(2):
@@ -320,13 +328,12 @@ def tile_rwkv_timemix_pa_t_kernel(
 
         h_words, h_mx = {}, {}
 
-        def make_h(g, i, on_vector):
+        def make_h(g, i):
             h_words[g, i] = back.tile([P, P, PACK], BF16, tag="h_words", name="h_words", bufs=3, align_bytes=64)
-            engine = nc.vector if on_vector else nc.gpsimd
-            engine.tensor_mul(
-                out=h_words[g, i][:],
-                in0=wkv_planes[g][:, :, P * i : P * (i + 1)].rearrange("p t k -> p k t"),
-                in1=r_planes[g][:, :, P * i : P * (i + 1)].rearrange("p t k -> p k t"),
+            nc.vector.tensor_mul(
+                out=h_words[g, i][:].rearrange("p (c i) t -> p c t i", i=4),
+                in0=wkv_planes[g][:, :, P * i : P * (i + 1)].rearrange("p t (c i) -> p c t i", i=4),
+                in1=r_planes[g][:, :, P * i : P * (i + 1)].rearrange("p t (c i) -> p c t i", i=4),
             )
 
         def quantise_h(g, i):
@@ -339,11 +346,16 @@ def tile_rwkv_timemix_pa_t_kernel(
             )
             h_mx[g, i] = (codes, plane)
 
-        def project(g, i, on_vector):
+        o_accs = {}
+
+        def project(g, i, cooling_down):
             codes, plane = h_mx[g, i]
-            o_acc = psum.tile([P, C], F32, tag="o")
+            if cooling_down:
+                o_accs[g, i] = psum.tile([P, C], F32, tag="step", name="o_acc", bufs=2)
+            else:
+                o_accs[g, i] = psum.tile([P, C], F32, tag="o", name="o_acc")
             nc.tensor.matmul_mx(
-                out=o_acc[:],
+                out=o_accs[g, i][:],
                 lhsT=codes[:].bitcast(FP8X4),
                 lhsT_scale=plane[:],
                 rhs=arrived_codes[:, W_OUT, :].bitcast(FP8X4),
@@ -351,8 +363,10 @@ def tile_rwkv_timemix_pa_t_kernel(
                 start=True,
                 stop=True,
             )
+
+        def store(g, i, on_vector):
             o_sb = back.tile([P, C], F32, tag="o_sb", bufs=3)
-            copy(on_vector, o_sb[:], o_acc[:])
+            copy(on_vector, o_sb[:], o_accs[g, i][:])
             nc.sync.dma_start(out=out[g, P * i : P * (i + 1), :], in_=o_sb[:])
 
         def is_sequence(q):
@@ -371,45 +385,49 @@ def tile_rwkv_timemix_pa_t_kernel(
             if n == PERMUTE_STEP:
                 permute_columns()
 
-            f, part = divmod(n - PROJECT_LAG, TOK_TILES)
+            f, part = divmod(n - H_LAG, TOK_TILES)
             if is_sequence(f):
-                project(f, part, cooling_down and part % 2 == 1)
+                make_h(f, part)
+            f, part = divmod(n - QUANTISE_H_LAG, TOK_TILES)
+            if is_sequence(f):
+                quantise_h(f, part)
+                project(f, part, cooling_down)
+            f, part = divmod(n + QUANTISE_LEAD, PACK)
+            if is_sequence(f) and part < 3:
+                quantise_mix(f, MIX_ORDER[part])
+
             if is_unit(n + 1):
                 stage1(n + 1, W_K)
                 stage1(n + 1, W_R)
                 stage1(n + 1, W_V)
             if is_unit(n):
                 make_bracket(n)
+
+            f, part = divmod(n + REGROUP_LEAD, PACK)
+            if is_sequence(f) and part < 3:
+                regroup_mix(f, MIX_ORDER[part], warming_up)
+            f, part = divmod(n - PROJECT_LAG, TOK_TILES)
+            if is_sequence(f):
+                store(f, part, cooling_down and part % 2 == 1)
             if is_unit(n + 1):
                 gates_without_k(n + 1)
 
             f, part = divmod(n + TRANSPOSE_LEAD, PACK)
             if is_sequence(f) and part < 2:
                 transpose_x(f, part, warming_up)
+            if n == FIRST_STEP:
+                per_channel_numbers()
             f, part = divmod(n + DIFFERENCE_LEAD, PACK)
             if is_sequence(f):
                 difference_plane(f, part)
             f, part = divmod(n + MIX_LEAD, PACK)
             if is_sequence(f):
                 mix_plane(f, part)
-            f, part = divmod(n + REGROUP_LEAD, PACK)
-            if is_sequence(f) and part < 3:
-                regroup_mix(f, MIX_ORDER[part], warming_up)
 
             if is_unit(n + 1):
                 make_logit(n + 1)
                 gate_ns(n + 1)
-            f, part = divmod(n - H_LAG, TOK_TILES)
-            if is_sequence(f):
-                make_h(f, part, cooling_down)
             if is_unit(n):
                 make_wkv(n)
-
-            f, part = divmod(n + QUANTISE_LEAD, PACK)
-            if is_sequence(f) and part < 3:
-                quantise_mix(f, MIX_ORDER[part])
-            f, part = divmod(n - QUANTISE_H_LAG, TOK_TILES)
-            if is_sequence(f):
-                quantise_h(f, part)
             if is_sequence(n + LN_BETA_LEAD):
                 make_ln_beta(n + LN_BETA_LEAD)

@@ -33,17 +33,19 @@ W_R, W_K, W_V, W_OUT = 0, 1, 2, 3
 UNITS = B * PACK
 MIX_ORDER = (W_K, W_V, W_R)
 
-LOAD_LEAD = 13
-TRANSPOSE_LEAD = 11
+LOAD_LEAD = 14
+LOADED_AT_START = 2
+TRANSPOSE_LEAD = 12
 DIFFERENCE_LEAD = 10
 MIX_LEAD = 9
 REGROUP_LEAD = 5
 QUANTISE_LEAD = 4
 LN_BETA_LEAD = B + 1
 PERMUTE_STEP = -9
-H_LAG = 4
-QUANTISE_H_LAG = 5
-PROJECT_LAG = 5
+WKV_LAG = 1
+H_LAG = 5
+QUANTISE_H_LAG = 6
+PROJECT_LAG = 6
 FIRST_STEP = -TRANSPOSE_LEAD
 LAST_STEP = UNITS - PACK + PROJECT_LAG + TOK_TILES
 
@@ -99,6 +101,8 @@ def tile_rwkv_timemix_pa_t_kernel(
             (nc.scalar, ROW_MU + 2, mu_v),
         ):
             queue.dma_start(out=rows[row : row + 1, :], in_=vector.unsqueeze(0))
+
+        load_x(1)
 
         arrived_codes = const.tile([P, 4, PACK * C], U8, align_bytes=64)
         arrived_planes = const.tile([P, 4, C], U8, align_bytes=64)
@@ -210,7 +214,8 @@ def tile_rwkv_timemix_pa_t_kernel(
             copy(on_vector, x_planes[f][:, 2 * pair : 2 * pair + 2, 2 : T + 2], xt[:])
 
         def difference_plane(f, t):
-            steps[f, t] = psum.tile([P, T], F32, tag="step", name="step", bufs=2)
+            spare_bank = t % 2 == 1 and PACK * f - MIX_LEAD + t < PROJECT_LAG
+            steps[f, t] = psum.tile([P, T], F32, tag="o" if spare_bank else "step", name="step")
             for i in range(TOK_TILES):
                 nc.tensor.matmul(
                     out=steps[f, t][:, P * i : P * (i + 1)],
@@ -246,13 +251,23 @@ def tile_rwkv_timemix_pa_t_kernel(
                     op1=ALU.add,
                 )
 
-        def regroup_mix(f, mix, on_vector):
-            mixed[f, mix] = front.tile([P, T, PACK], BF16, tag="mixed", name="mixed", align_bytes=64)
-            copy(
-                on_vector,
-                mixed[f, mix][:].rearrange("p (c i) t -> p c t i", i=4),
-                mixed_planes[f, mix][:].rearrange("p t (c i) -> p c t i", i=4),
-            )
+        def regroup_mix(f, mix, on_gpsimd):
+            if on_gpsimd:
+                mixed[f, mix] = front.tile([P, T, PACK], BF16, tag="mixed_early", name="mixed", bufs=1, align_bytes=64)
+                nc.gpsimd.tensor_scalar(
+                    out=mixed[f, mix][:],
+                    in0=mixed_planes[f, mix][:].rearrange("p t k -> p k t"),
+                    scalar1=1.0,
+                    scalar2=0.0,
+                    op0=ALU.mult,
+                    op1=ALU.add,
+                )
+            else:
+                mixed[f, mix] = front.tile([P, T, PACK], BF16, tag="mixed", name="mixed", align_bytes=64)
+                nc.scalar.copy(
+                    out=mixed[f, mix][:].rearrange("p (c i) t -> p c t i", i=4),
+                    in_=mixed_planes[f, mix][:].rearrange("p t (c i) -> p c t i", i=4),
+                )
 
         def quantise_mix(f, mix):
             codes = front.tile([P, T], U32, tag="codes%d" % mix, align_bytes=64)
@@ -269,7 +284,7 @@ def tile_rwkv_timemix_pa_t_kernel(
         def stage1(n, which):
             b, t = divmod(n, PACK)
             codes, plane = mixes[b, which]
-            acc[n, which] = psum.tile([P, T], F32, tag="acc%d" % which, name="acc", bufs=2 if which == W_V else 1)
+            acc[n, which] = psum.tile([P, T], F32, tag="acc%d" % which, name="acc", bufs=3 if which == W_V else 1)
             nc.tensor.matmul_mx(
                 out=acc[n, which][:],
                 lhsT=w_codes[:, which, PACK * P * t : PACK * P * (t + 1)].bitcast(FP8X4),
@@ -318,7 +333,8 @@ def tile_rwkv_timemix_pa_t_kernel(
                 op1=ALU.add,
             )
             ns_bracket[n] = back.tile([P, T], F32, tag="ns_bracket", name="ns_bracket")
-            nc.gpsimd.tensor_mul(out=ns_bracket[n][:], in0=bracket[n][:], in1=ns[n][:])
+            engine = nc.vector if n == UNITS - 1 else nc.gpsimd
+            engine.tensor_mul(out=ns_bracket[n][:], in0=bracket[n][:], in1=ns[n][:])
 
         def make_wkv(n):
             b, t = divmod(n, PACK)
@@ -350,8 +366,8 @@ def tile_rwkv_timemix_pa_t_kernel(
 
         def project(g, i, cooling_down):
             codes, plane = h_mx[g, i]
-            if cooling_down:
-                o_accs[g, i] = psum.tile([P, C], F32, tag="step", name="o_acc", bufs=2)
+            if cooling_down and i % 2 == 1:
+                o_accs[g, i] = psum.tile([P, C], F32, tag="step", name="o_acc")
             else:
                 o_accs[g, i] = psum.tile([P, C], F32, tag="o", name="o_acc")
             nc.tensor.matmul_mx(
@@ -364,9 +380,9 @@ def tile_rwkv_timemix_pa_t_kernel(
                 stop=True,
             )
 
-        def store(g, i, on_vector):
+        def store(g, i):
             o_sb = back.tile([P, C], F32, tag="o_sb", bufs=3)
-            copy(on_vector, o_sb[:], o_accs[g, i][:])
+            nc.scalar.copy(out=o_sb[:], in_=o_accs[g, i][:])
             nc.sync.dma_start(out=out[g, P * i : P * (i + 1), :], in_=o_sb[:])
 
         def is_sequence(q):
@@ -380,7 +396,7 @@ def tile_rwkv_timemix_pa_t_kernel(
             cooling_down = n >= UNITS
 
             f, part = divmod(n + LOAD_LEAD, PACK)
-            if is_sequence(f) and part == 0:
+            if is_sequence(f) and part == 0 and f >= LOADED_AT_START:
                 load_x(f)
             if n == PERMUTE_STEP:
                 permute_columns()
@@ -402,13 +418,15 @@ def tile_rwkv_timemix_pa_t_kernel(
                 stage1(n + 1, W_V)
             if is_unit(n):
                 make_bracket(n)
+            if is_unit(n - WKV_LAG):
+                make_wkv(n - WKV_LAG)
 
             f, part = divmod(n + REGROUP_LEAD, PACK)
             if is_sequence(f) and part < 3:
                 regroup_mix(f, MIX_ORDER[part], warming_up)
             f, part = divmod(n - PROJECT_LAG, TOK_TILES)
             if is_sequence(f):
-                store(f, part, cooling_down and part % 2 == 1)
+                store(f, part)
             if is_unit(n + 1):
                 gates_without_k(n + 1)
 
@@ -417,17 +435,15 @@ def tile_rwkv_timemix_pa_t_kernel(
                 transpose_x(f, part, warming_up)
             if n == FIRST_STEP:
                 per_channel_numbers()
-            f, part = divmod(n + DIFFERENCE_LEAD, PACK)
-            if is_sequence(f):
-                difference_plane(f, part)
             f, part = divmod(n + MIX_LEAD, PACK)
             if is_sequence(f):
                 mix_plane(f, part)
+            f, part = divmod(n + DIFFERENCE_LEAD, PACK)
+            if is_sequence(f):
+                difference_plane(f, part)
 
             if is_unit(n + 1):
                 make_logit(n + 1)
                 gate_ns(n + 1)
-            if is_unit(n):
-                make_wkv(n)
             if is_sequence(n + LN_BETA_LEAD):
                 make_ln_beta(n + LN_BETA_LEAD)

@@ -40,8 +40,8 @@ DIFFERENCE_LEAD = 10
 MIX_LEAD = 9
 REGROUP_LEAD = 5
 QUANTISE_LEAD = 4
+LAST_MOVE_STEP = -REGROUP_LEAD + 2
 LN_BETA_LEAD = B + 1
-PERMUTE_STEP = -9
 WKV_LAG = 1
 H_LAG = 5
 QUANTISE_H_LAG = 6
@@ -82,11 +82,11 @@ def tile_rwkv_timemix_pa_t_kernel(
 
         x_rows = {}
 
-        def load_x(f):
+        def load_x(f, queue):
             x_rows[f] = front.tile([P, TOK_TILES, C], BF16, tag="x_rows", name="x_rows")
-            nc.sync.dma_start(out=x_rows[f][:], in_=x[f].rearrange("(i p) c -> p i c", p=P))
+            queue.dma_start(out=x_rows[f][:], in_=x[f].rearrange("(i p) c -> p i c", p=P))
 
-        load_x(0)
+        load_x(0, nc.sync)
 
         rows = const.tile([P, C], BF16)
         nc.vector.memset(rows[:], 0.0)
@@ -102,7 +102,7 @@ def tile_rwkv_timemix_pa_t_kernel(
         ):
             queue.dma_start(out=rows[row : row + 1, :], in_=vector.unsqueeze(0))
 
-        load_x(1)
+        load_x(1, nc.scalar)
 
         arrived_codes = const.tile([P, 4, PACK * C], U8, align_bytes=64)
         arrived_planes = const.tile([P, 4, C], U8, align_bytes=64)
@@ -127,16 +127,17 @@ def tile_rwkv_timemix_pa_t_kernel(
         w_codes = const.tile([P, 3, PACK * C], U8, align_bytes=64)
         w_planes = const.tile([P, 3, C], U8, align_bytes=64)
 
-        def permute_columns():
-            for wi in (W_K, W_R, W_V):
-                nc.gpsimd.tensor_copy(
-                    out=w_codes[:, wi, :].bitcast(I32).rearrange("p (t m) -> p t m", t=PACK),
-                    in_=arrived_codes[:, wi, :].bitcast(I32).rearrange("p (m t) -> p t m", t=PACK),
-                )
-                nc.gpsimd.tensor_copy(
-                    out=w_planes[:, wi, :].rearrange("p (t m) -> p m t", t=PACK),
-                    in_=arrived_planes[:, wi, :].rearrange("p (m t) -> p m t", t=PACK),
-                )
+        def move_codes(wi):
+            nc.gpsimd.tensor_copy(
+                out=w_codes[:, wi, :].bitcast(I32).rearrange("p (t m) -> p t m", t=PACK),
+                in_=arrived_codes[:, wi, :].bitcast(I32).rearrange("p (m t) -> p t m", t=PACK),
+            )
+
+        def move_scales(wi):
+            nc.gpsimd.tensor_copy(
+                out=w_planes[:, wi, :].rearrange("p (t m) -> p m t", t=PACK),
+                in_=arrived_planes[:, wi, :].rearrange("p (m t) -> p m t", t=PACK),
+            )
 
         ident_bf16 = const.tile([P, P], BF16)
         make_identity(nc, ident_bf16[:])
@@ -165,6 +166,11 @@ def tile_rwkv_timemix_pa_t_kernel(
         b0_inverse = const.tile([P, PACK, B], F32)
         ln_beta = const.tile([P, B, PACK, T], F32)
         decay = back.tile([P, PACK, T], F32, tag="r_planes", bufs=3)
+
+        for wi in (W_R, W_K, W_V):
+            move_codes(wi)
+        move_scales(W_R)
+        move_scales(W_K)
 
         def per_channel_numbers():
             rows_t = psum.tile([P, PACK, P], BF16, tag="o")
@@ -344,9 +350,13 @@ def tile_rwkv_timemix_pa_t_kernel(
 
         h_words, h_mx = {}, {}
 
-        def make_h(g, i):
-            h_words[g, i] = back.tile([P, P, PACK], BF16, tag="h_words", name="h_words", bufs=3, align_bytes=64)
-            nc.vector.tensor_mul(
+        def make_h(g, i, on_vector):
+            if on_vector:
+                h_words[g, i] = back.tile([P, P, PACK], BF16, tag="h_words_late", name="h_words", align_bytes=64)
+            else:
+                h_words[g, i] = back.tile([P, P, PACK], BF16, tag="h_words", name="h_words", bufs=1, align_bytes=64)
+            engine = nc.vector if on_vector else nc.gpsimd
+            engine.tensor_mul(
                 out=h_words[g, i][:].rearrange("p (c i) t -> p c t i", i=4),
                 in0=wkv_planes[g][:, :, P * i : P * (i + 1)].rearrange("p t (c i) -> p c t i", i=4),
                 in1=r_planes[g][:, :, P * i : P * (i + 1)].rearrange("p t (c i) -> p c t i", i=4),
@@ -380,9 +390,9 @@ def tile_rwkv_timemix_pa_t_kernel(
                 stop=True,
             )
 
-        def store(g, i):
+        def store(g, i, on_vector):
             o_sb = back.tile([P, C], F32, tag="o_sb", bufs=3)
-            nc.scalar.copy(out=o_sb[:], in_=o_accs[g, i][:])
+            copy(on_vector, o_sb[:], o_accs[g, i][:])
             nc.sync.dma_start(out=out[g, P * i : P * (i + 1), :], in_=o_sb[:])
 
         def is_sequence(q):
@@ -397,20 +407,21 @@ def tile_rwkv_timemix_pa_t_kernel(
 
             f, part = divmod(n + LOAD_LEAD, PACK)
             if is_sequence(f) and part == 0 and f >= LOADED_AT_START:
-                load_x(f)
-            if n == PERMUTE_STEP:
-                permute_columns()
+                load_x(f, nc.sync)
 
+            f, part = divmod(n + QUANTISE_LEAD, PACK)
+            if is_sequence(f) and part < 3:
+                quantise_mix(f, MIX_ORDER[part])
             f, part = divmod(n - H_LAG, TOK_TILES)
-            if is_sequence(f):
-                make_h(f, part)
+            if is_sequence(f) and cooling_down:
+                make_h(f, part, True)
             f, part = divmod(n - QUANTISE_H_LAG, TOK_TILES)
             if is_sequence(f):
                 quantise_h(f, part)
                 project(f, part, cooling_down)
-            f, part = divmod(n + QUANTISE_LEAD, PACK)
-            if is_sequence(f) and part < 3:
-                quantise_mix(f, MIX_ORDER[part])
+            f, part = divmod(n - H_LAG, TOK_TILES)
+            if is_sequence(f) and not cooling_down:
+                make_h(f, part, False)
 
             if is_unit(n + 1):
                 stage1(n + 1, W_K)
@@ -424,9 +435,11 @@ def tile_rwkv_timemix_pa_t_kernel(
             f, part = divmod(n + REGROUP_LEAD, PACK)
             if is_sequence(f) and part < 3:
                 regroup_mix(f, MIX_ORDER[part], warming_up)
+            if n == LAST_MOVE_STEP:
+                move_scales(W_V)
             f, part = divmod(n - PROJECT_LAG, TOK_TILES)
             if is_sequence(f):
-                store(f, part)
+                store(f, part, part % 2 == 1 and not cooling_down)
             if is_unit(n + 1):
                 gates_without_k(n + 1)
 

@@ -46,6 +46,8 @@ WKV_LAG = 1
 H_LAG = 5
 QUANTISE_H_LAG = 6
 PROJECT_LAG = 6
+LAST_MIX_STEP = PACK * (B - 1) - MIX_LEAD + PACK - 1
+LAST_REGROUP_STEP = PACK * (B - 1) - REGROUP_LEAD + len(MIX_ORDER) - 1
 FIRST_STEP = -TRANSPOSE_LEAD
 LAST_STEP = UNITS - PACK + PROJECT_LAG + TOK_TILES
 
@@ -403,6 +405,8 @@ def tile_rwkv_timemix_pa_t_kernel(
 
         for n in range(FIRST_STEP, LAST_STEP):
             warming_up = n < 0
+            after_gpsimd = n + QUANTISE_LEAD - REGROUP_LEAD < 0
+            mixing = n <= LAST_MIX_STEP
             cooling_down = n >= UNITS
 
             f, part = divmod(n + LOAD_LEAD, PACK)
@@ -410,17 +414,17 @@ def tile_rwkv_timemix_pa_t_kernel(
                 load_x(f, nc.sync)
 
             f, part = divmod(n + QUANTISE_LEAD, PACK)
-            if is_sequence(f) and part < 3:
+            if is_sequence(f) and part < 3 and not after_gpsimd:
                 quantise_mix(f, MIX_ORDER[part])
             f, part = divmod(n - H_LAG, TOK_TILES)
-            if is_sequence(f) and cooling_down:
+            if is_sequence(f) and not mixing:
                 make_h(f, part, True)
             f, part = divmod(n - QUANTISE_H_LAG, TOK_TILES)
             if is_sequence(f):
                 quantise_h(f, part)
                 project(f, part, cooling_down)
             f, part = divmod(n - H_LAG, TOK_TILES)
-            if is_sequence(f) and not cooling_down:
+            if is_sequence(f) and mixing:
                 make_h(f, part, False)
 
             if is_unit(n + 1):
@@ -433,13 +437,11 @@ def tile_rwkv_timemix_pa_t_kernel(
                 make_wkv(n - WKV_LAG)
 
             f, part = divmod(n + REGROUP_LEAD, PACK)
-            if is_sequence(f) and part < 3:
+            if is_sequence(f) and part < 3 and (part == 0 or not warming_up):
                 regroup_mix(f, MIX_ORDER[part], warming_up)
-            if n == LAST_MOVE_STEP:
-                move_scales(W_V)
             f, part = divmod(n - PROJECT_LAG, TOK_TILES)
             if is_sequence(f):
-                store(f, part, part % 2 == 1 and not cooling_down)
+                store(f, part, part % 2 == 1 if mixing else n <= LAST_REGROUP_STEP)
             if is_unit(n + 1):
                 gates_without_k(n + 1)
 
@@ -454,6 +456,15 @@ def tile_rwkv_timemix_pa_t_kernel(
             f, part = divmod(n + DIFFERENCE_LEAD, PACK)
             if is_sequence(f):
                 difference_plane(f, part)
+
+            f, part = divmod(n + QUANTISE_LEAD, PACK)
+            if is_sequence(f) and part < 3 and after_gpsimd:
+                quantise_mix(f, MIX_ORDER[part])
+            f, part = divmod(n + REGROUP_LEAD, PACK)
+            if is_sequence(f) and 0 < part < 3 and warming_up:
+                regroup_mix(f, MIX_ORDER[part], True)
+            if n == LAST_MOVE_STEP:
+                move_scales(W_V)
 
             if is_unit(n + 1):
                 make_logit(n + 1)

@@ -137,12 +137,14 @@ def tile_rwkv_timemix_pa_t_kernel(
 
         def move_scales(wi):
             nc.gpsimd.tensor_copy(
-                out=w_planes[:, wi, :].rearrange("p (t m) -> p m t", t=PACK),
-                in_=arrived_planes[:, wi, :].rearrange("p (m t) -> p m t", t=PACK),
+                out=w_planes[:, wi, :].rearrange("p (t m) -> p t m", t=PACK),
+                in_=arrived_planes[:, wi, :].rearrange("p (m t) -> p t m", t=PACK),
             )
 
         ident_bf16 = const.tile([P, P], BF16)
         make_identity(nc, ident_bf16[:])
+        ident_f32 = const.tile([P, P], F32)
+        make_identity(nc, ident_f32[:])
 
         difference = const.tile([P, P], BF16)
         nc.vector.tensor_copy(out=difference[:], in_=ident_bf16[:])
@@ -198,7 +200,7 @@ def tile_rwkv_timemix_pa_t_kernel(
                     bias=eps_col[:],
                 )
 
-        x_planes, steps, mixed_planes, mixed, mixes = {}, {}, {}, {}, {}
+        x_pairs, steps, mixed_planes, mixed, mixes = {}, {}, {}, {}, {}
 
         def copy(on_vector, dst, src):
             if on_vector:
@@ -208,18 +210,23 @@ def tile_rwkv_timemix_pa_t_kernel(
 
         def transpose_x(f, pair, on_vector):
             if pair == 0:
-                x_planes[f] = front.tile([P, PACK, T + 2], BF16, tag="x_planes", name="x_planes")
+                x_pairs[f] = front.tile([P, 2, T + 1], F32, tag="x_pairs", name="x_pairs")
             else:
-                copy(on_vector, x_planes[f][:, :, 1], cols[:, :, ROW_XPREV + f])
-            xt = psum.tile([P, 2, T], BF16, tag="xt")
-            for e in range(2):
-                for i in range(TOK_TILES):
-                    nc.tensor.transpose(
-                        xt[:, e, P * i : P * (i + 1)],
-                        x_rows[f][:, i, 2 * pair + e : C : PACK],
-                        ident_bf16[:],
-                    )
-            copy(on_vector, x_planes[f][:, 2 * pair : 2 * pair + 2, 2 : T + 2], xt[:])
+                copy(
+                    on_vector,
+                    x_pairs[f][:].rearrange("p u k -> p (u k)").bitcast(BF16).rearrange(
+                        "p (u k e) -> p u k e", u=2, e=2
+                    )[:, :, 0, :],
+                    cols[:, :, ROW_XPREV + f].rearrange("p (u e) -> p u e", e=2),
+                )
+            xt = psum.tile([P, T], F32, tag="xt")
+            for i in range(TOK_TILES):
+                nc.tensor.transpose(
+                    xt[:, P * i : P * (i + 1)],
+                    x_rows[f][:, i, :].bitcast(F32)[:, pair : C // 2 : 2],
+                    ident_f32[:],
+                )
+            copy(on_vector, x_pairs[f][:, pair, 1 : T + 1], xt[:])
 
         def difference_plane(f, t):
             spare_bank = t % 2 == 1 and PACK * f - MIX_LEAD + t < PROJECT_LAG
@@ -254,7 +261,7 @@ def tile_rwkv_timemix_pa_t_kernel(
                     out=mixed_planes[f, mix][:, t, :],
                     in0=steps[f, t][:],
                     scalar=cols[:, t, ROW_MU + mix : ROW_MU + mix + 1],
-                    in1=x_planes[f][:, t, 1 : T + 1],
+                    in1=x_pairs[f][:, t // 2, 0:T].bitcast(BF16)[:, t % 2 : 2 * T : 2],
                     op0=ALU.mult,
                     op1=ALU.add,
                 )
@@ -441,7 +448,7 @@ def tile_rwkv_timemix_pa_t_kernel(
                 regroup_mix(f, MIX_ORDER[part], warming_up)
             f, part = divmod(n - PROJECT_LAG, TOK_TILES)
             if is_sequence(f):
-                store(f, part, part % 2 == 1 if mixing else n <= LAST_REGROUP_STEP)
+                store(f, part, (n + QUANTISE_LEAD) % PACK == len(MIX_ORDER) if mixing else n <= LAST_REGROUP_STEP)
             if is_unit(n + 1):
                 gates_without_k(n + 1)
 

@@ -21,12 +21,10 @@ EPS = 1e-8
 FLOPS = 4 * 2 * B * T * C * C
 
 ROW_A0 = 0
-ROW_B0 = 8
-ROW_XPREV = 16
-ROW_W = 24
-ROW_U = 25
-ROW_MU = 26
-ROWS = 32
+ROW_XPREV = 8
+ROW_U = 16
+ROW_MU = 17
+ROWS = 20
 
 W_R, W_K, W_V, W_OUT = 0, 1, 2, 3
 
@@ -90,17 +88,25 @@ def tile_rwkv_timemix_pa_t_kernel(
 
         load_x(0, nc.sync)
 
+        warm_in = const.tile([P, 1], F32)
+        warm_out = const.tile([P, 1], F32)
+        nc.gpsimd.memset(warm_in[:], 0.0)
+        nc.scalar.activation(out=warm_out[:], in_=warm_in[:], func=ACT.Exp)
+
+        w_bf16 = const.tile([P, PACK], BF16)
+        b0_bf16 = const.tile([P, B, PACK], BF16)
+        nc.scalar.dma_start(out=w_bf16[:], in_=w.rearrange("(p t) -> p t", t=PACK))
+        nc.scalar.dma_start(out=b0_bf16[:], in_=b0.rearrange("b (p t) -> p b t", t=PACK))
+
         rows = const.tile([P, C], BF16)
         nc.vector.memset(rows[:], 0.0)
-        nc.sync.dma_start(out=rows[ROW_B0 : ROW_B0 + B, :], in_=b0)
         nc.scalar.dma_start(out=rows[ROW_XPREV : ROW_XPREV + B, :], in_=x_prev0)
         nc.sync.dma_start(out=rows[ROW_A0 : ROW_A0 + B, :], in_=a0)
         for queue, row, vector in (
-            (nc.sync, ROW_W, w),
-            (nc.scalar, ROW_MU, mu_r),
-            (nc.sync, ROW_U, u),
+            (nc.sync, ROW_MU, mu_r),
             (nc.scalar, ROW_MU + 1, mu_k),
-            (nc.scalar, ROW_MU + 2, mu_v),
+            (nc.sync, ROW_MU + 2, mu_v),
+            (nc.scalar, ROW_U, u),
         ):
             queue.dma_start(out=rows[row : row + 1, :], in_=vector.unsqueeze(0))
 
@@ -161,15 +167,20 @@ def tile_rwkv_timemix_pa_t_kernel(
 
         cols = const.tile([P, PACK, ROWS], F32)
         a0_col = cols[:, :, ROW_A0 : ROW_A0 + B]
-        b0_col = cols[:, :, ROW_B0 : ROW_B0 + B]
-        negated = const.tile([P, PACK, 2], F32)
-        neg_w = negated[:, :, 0]
-        neg_u = negated[:, :, 1]
+        b0_col = const.tile([P, PACK, B], F32)
+        neg_w = const.tile([P, PACK], F32)
+        neg_u = const.tile([P, PACK], F32)
         chi_bias = const.tile([P, PACK, B], F32)
         neg_alpha = const.tile([P, PACK, B], F32)
         b0_inverse = const.tile([P, PACK, B], F32)
         ln_beta = const.tile([P, B, PACK, T], F32)
         decay = back.tile([P, PACK, T], F32, tag="r_planes", bufs=3)
+        nc.vector.tensor_scalar_mul(out=neg_w[:], in0=w_bf16[:], scalar1=-1.0)
+        nc.vector.tensor_copy(out=b0_col[:], in_=b0_bf16[:].rearrange("p b t -> p t b"))
+        for t in range(PACK):
+            nc.scalar.activation(out=decay[:, t, :], in_=counts[:], func=ACT.Exp, scale=neg_w[:, t : t + 1])
+        nc.scalar.activation(out=chi_bias[:], in_=b0_col[:], func=ACT.Ln, scale=1.0 / EPS)
+        nc.vector.reciprocal(b0_inverse[:], b0_col[:])
 
         for wi in (W_R, W_K, W_V):
             move_codes(wi)
@@ -181,11 +192,7 @@ def tile_rwkv_timemix_pa_t_kernel(
             for t in range(PACK):
                 nc.tensor.transpose(rows_t[:, t, :], rows[:, t:C:PACK], ident_bf16[:])
             nc.vector.tensor_copy(out=cols[:], in_=rows_t[:, :, 0:ROWS])
-            nc.vector.tensor_scalar_mul(out=negated[:], in0=cols[:, :, ROW_W : ROW_U + 1], scalar1=-1.0)
-            for t in range(PACK):
-                nc.scalar.activation(out=decay[:, t, :], in_=counts[:], func=ACT.Exp, scale=neg_w[:, t : t + 1])
-            nc.scalar.activation(out=chi_bias[:], in_=b0_col, func=ACT.Ln, scale=1.0 / EPS)
-            nc.vector.reciprocal(b0_inverse[:], b0_col)
+            nc.vector.tensor_scalar_mul(out=neg_u[:], in0=cols[:, :, ROW_U], scalar1=-1.0)
             nc.vector.scalar_tensor_tensor(
                 out=neg_alpha[:], in0=a0_col, scalar=-1.0, in1=b0_inverse[:], op0=ALU.mult, op1=ALU.mult
             )
@@ -454,7 +461,7 @@ def tile_rwkv_timemix_pa_t_kernel(
 
             f, part = divmod(n + TRANSPOSE_LEAD, PACK)
             if is_sequence(f) and part < 2:
-                transpose_x(f, part, warming_up)
+                transpose_x(f, part, f == 0)
             if n == FIRST_STEP:
                 per_channel_numbers()
             f, part = divmod(n + MIX_LEAD, PACK)

@@ -28,6 +28,8 @@ ROWS = 20
 
 W_R, W_K, W_V, W_OUT = 0, 1, 2, 3
 
+FRONT_BANKS = ("step", "o", "xt")
+
 UNITS = B * PACK
 MIX_ORDER = (W_K, W_V, W_R)
 
@@ -43,11 +45,11 @@ LN_BETA_LEAD = B + 1
 WKV_LAG = 1
 H_LAG = 5
 QUANTISE_H_LAG = 6
-PROJECT_LAG = 6
 LAST_MIX_STEP = PACK * (B - 1) - MIX_LEAD + PACK - 1
 LAST_REGROUP_STEP = PACK * (B - 1) - REGROUP_LEAD + len(MIX_ORDER) - 1
+HELD_SLICES = LAST_MIX_STEP + 1 - QUANTISE_H_LAG + 1
 FIRST_STEP = -TRANSPOSE_LEAD
-LAST_STEP = UNITS - PACK + PROJECT_LAG + TOK_TILES
+LAST_STEP = UNITS - PACK + QUANTISE_H_LAG + TOK_TILES + 1
 
 
 def tile_rwkv_timemix_pa_t_kernel(
@@ -158,7 +160,7 @@ def tile_rwkv_timemix_pa_t_kernel(
         neg_ident = const.tile([P, P], BF16)
         nc.vector.tensor_scalar_mul(out=neg_ident[:], in0=ident_bf16[:], scalar1=-1.0)
 
-        counts_i32 = back.tile([P, T], I32, tag="o_sb", bufs=3)
+        counts_i32 = back.tile([P, T], I32, tag="o_sb", bufs=4)
         nc.gpsimd.iota(counts_i32[:], pattern=[[1, T]], base=1, channel_multiplier=0)
         counts = const.tile([P, T], F32)
         nc.vector.tensor_copy(out=counts[:], in_=counts_i32[:])
@@ -236,8 +238,7 @@ def tile_rwkv_timemix_pa_t_kernel(
             copy(on_vector, x_pairs[f][:, pair, 1 : T + 1], xt[:])
 
         def difference_plane(f, t):
-            spare_bank = t % 2 == 1 and PACK * f - MIX_LEAD + t < PROJECT_LAG
-            steps[f, t] = psum.tile([P, T], F32, tag="o" if spare_bank else "step", name="step")
+            steps[f, t] = psum.tile([P, T], F32, tag=FRONT_BANKS[t % 2], name="step")
             for i in range(TOK_TILES):
                 nc.tensor.matmul(
                     out=steps[f, t][:, P * i : P * (i + 1)],
@@ -379,8 +380,8 @@ def tile_rwkv_timemix_pa_t_kernel(
             )
 
         def quantise_h(g, i):
-            codes = back.tile([P, P], U32, tag="h_codes", bufs=3, align_bytes=64)
-            plane = back.tile([P, P], U8, tag="h_plane", bufs=3, align_bytes=64)
+            codes = back.tile([P, P], U32, tag="h_codes", bufs=HELD_SLICES, align_bytes=64)
+            plane = back.tile([P, P], U8, tag="h_plane", bufs=HELD_SLICES, align_bytes=64)
             nc.vector.quantize_mx(
                 out=codes[:].bitcast(FP8X4),
                 scales=plane[:],
@@ -390,12 +391,9 @@ def tile_rwkv_timemix_pa_t_kernel(
 
         o_accs = {}
 
-        def project(g, i, cooling_down):
+        def project(g, i, bank):
             codes, plane = h_mx[g, i]
-            if cooling_down and i % 2 == 1:
-                o_accs[g, i] = psum.tile([P, C], F32, tag="step", name="o_acc")
-            else:
-                o_accs[g, i] = psum.tile([P, C], F32, tag="o", name="o_acc")
+            o_accs[g, i] = psum.tile([P, C], F32, tag=bank, name="o_acc")
             nc.tensor.matmul_mx(
                 out=o_accs[g, i][:],
                 lhsT=codes[:].bitcast(FP8X4),
@@ -406,8 +404,11 @@ def tile_rwkv_timemix_pa_t_kernel(
                 stop=True,
             )
 
-        def store(g, i, on_vector):
-            o_sb = back.tile([P, C], F32, tag="o_sb", bufs=3)
+        def store(g, i, on_vector, borrowed):
+            if borrowed is None:
+                o_sb = back.tile([P, C], F32, tag="o_sb", bufs=4)
+            else:
+                o_sb = front.tile([P, C], F32, tag="mixed_planes%d" % borrowed, name="o_sb")
             copy(on_vector, o_sb[:], o_accs[g, i][:])
             nc.sync.dma_start(out=out[g, P * i : P * (i + 1), :], in_=o_sb[:])
 
@@ -416,6 +417,11 @@ def tile_rwkv_timemix_pa_t_kernel(
 
         def is_unit(n):
             return 0 <= n < UNITS
+
+        quantised = []
+        projected = 0
+        in_psum = []
+        stored = 0
 
         for n in range(FIRST_STEP, LAST_STEP):
             warming_up = n < 0
@@ -430,15 +436,16 @@ def tile_rwkv_timemix_pa_t_kernel(
             f, part = divmod(n + QUANTISE_LEAD, PACK)
             if is_sequence(f) and part < 3 and not after_gpsimd:
                 quantise_mix(f, MIX_ORDER[part])
+            h_on_vector = cooling_down or (not mixing and (n - LAST_MIX_STEP) % 2 == 1)
             f, part = divmod(n - H_LAG, TOK_TILES)
-            if is_sequence(f) and not mixing:
+            if is_sequence(f) and h_on_vector:
                 make_h(f, part, True)
             f, part = divmod(n - QUANTISE_H_LAG, TOK_TILES)
             if is_sequence(f):
                 quantise_h(f, part)
-                project(f, part, cooling_down)
+                quantised.append((f, part))
             f, part = divmod(n - H_LAG, TOK_TILES)
-            if is_sequence(f) and mixing:
+            if is_sequence(f) and not h_on_vector:
                 make_h(f, part, False)
 
             if is_unit(n + 1):
@@ -453,15 +460,31 @@ def tile_rwkv_timemix_pa_t_kernel(
             f, part = divmod(n + REGROUP_LEAD, PACK)
             if is_sequence(f) and part < 3 and (part == 0 or not warming_up):
                 regroup_mix(f, MIX_ORDER[part], warming_up)
-            f, part = divmod(n - PROJECT_LAG, TOK_TILES)
-            if is_sequence(f):
-                store(f, part, (n + QUANTISE_LEAD) % PACK == len(MIX_ORDER) if mixing else n <= LAST_REGROUP_STEP)
             if is_unit(n + 1):
                 gates_without_k(n + 1)
 
+            for k, (g, i) in enumerate(in_psum):
+                full = len(in_psum) == len(FRONT_BANKS)
+                on_vector = n <= LAST_REGROUP_STEP or (k == 0 and full) or n == LAST_STEP - 1
+                if n > LAST_REGROUP_STEP and stored % 2 == 1:
+                    store(g, i, on_vector, MIX_ORDER[stored // 2 % len(MIX_ORDER)])
+                else:
+                    store(g, i, on_vector, None)
+                stored += 1
+            if mixing:
+                due = 0
+            elif n < LAST_REGROUP_STEP:
+                due = 2
+            else:
+                due = len(FRONT_BANKS)
+            in_psum = quantised[projected : projected + due]
+            for k, (g, i) in enumerate(in_psum):
+                project(g, i, FRONT_BANKS[(projected + k) % len(FRONT_BANKS)])
+            projected += len(in_psum)
+
             f, part = divmod(n + TRANSPOSE_LEAD, PACK)
             if is_sequence(f) and part < 2:
-                transpose_x(f, part, f == 0)
+                transpose_x(f, part, f <= 1)
             if n == FIRST_STEP:
                 per_channel_numbers()
             f, part = divmod(n + MIX_LEAD, PACK)

@@ -436,7 +436,7 @@ def tile_rwkv_timemix_pa_t_kernel(
             f, part = divmod(n + QUANTISE_LEAD, PACK)
             if is_sequence(f) and part < 3 and not after_gpsimd:
                 quantise_mix(f, MIX_ORDER[part])
-            h_on_vector = cooling_down or (not mixing and (n - LAST_MIX_STEP) % 2 == 1)
+            h_on_vector = not mixing
             f, part = divmod(n - H_LAG, TOK_TILES)
             if is_sequence(f) and h_on_vector:
                 make_h(f, part, True)

from contextlib import ExitStack

import concourse.mybir as mybir
from concourse.masks import make_identity

F32 = mybir.dt.float32
BF16 = mybir.dt.bfloat16
I32 = mybir.dt.int32
U32 = mybir.dt.uint32
U8 = mybir.dt.uint8
FP8X4 = mybir.dt.float8_e4m3fn_x4
ALU = mybir.AluOpType
ACT = mybir.ActivationFunctionType

P = 128
PACK = 4
B, T, C = 8, 512, 512
TOK_TILES = T // P
EPS = 1e-8

FLOPS = 4 * 2 * B * T * C * C

ROW_A0 = 0
ROW_XPREV = 8
ROW_U = 16
ROW_MU = 17
ROWS = 20

W_R, W_K, W_V, W_OUT = 0, 1, 2, 3

FRONT_BANKS = ("step", "o", "xt")

UNITS = B * PACK
MIX_ORDER = (W_K, W_V, W_R)

LOAD_LEAD = 14
LOADED_AT_START = 2
TRANSPOSE_LEAD = 12
DIFFERENCE_LEAD = 10
MIX_LEAD = 9
REGROUP_LEAD = 5
QUANTISE_LEAD = 4
LAST_MOVE_STEP = -REGROUP_LEAD + 2
LN_BETA_LEAD = B + 1
WKV_LAG = 1
H_LAG = 5
QUANTISE_H_LAG = 6
LAST_MIX_STEP = PACK * (B - 1) - MIX_LEAD + PACK - 1
LAST_REGROUP_STEP = PACK * (B - 1) - REGROUP_LEAD + len(MIX_ORDER) - 1
HELD_SLICES = LAST_MIX_STEP + 1 - QUANTISE_H_LAG + 1
FIRST_STEP = -TRANSPOSE_LEAD
LAST_STEP = UNITS - PACK + QUANTISE_H_LAG + TOK_TILES + 1


def tile_rwkv_timemix_pa_t_kernel(
    tc,
    x,
    a0,
    b0,
    x_prev0,
    w,
    u,
    mu_r,
    mu_k,
    mu_v,
    W_r_words,
    W_r_scales,
    W_k_words,
    W_k_scales,
    W_v_words,
    W_v_scales,
    W_out_words,
    W_out_scales,
    out,
):
    nc = tc.nc
    with ExitStack() as stack:
        const = stack.enter_context(tc.tile_pool(name="const", bufs=1))
        front = stack.enter_context(tc.tile_pool(name="front", bufs=2))
        back = stack.enter_context(tc.tile_pool(name="back", bufs=2))
        psum = stack.enter_context(tc.psum_pool(name="psum", bufs=1))

        stack.enter_context(tc.manual_schedule())

        x_rows = {}

        def load_x(f, queue):
            x_rows[f] = front.tile([P, TOK_TILES, C], BF16, tag="x_rows", name="x_rows")
            queue.dma_start(out=x_rows[f][:], in_=x[f].rearrange("(i p) c -> p i c", p=P))

        load_x(0, nc.sync)

        warm_in = const.tile([P, 1], F32)
        warm_out = const.tile([P, 1], F32)
        nc.gpsimd.memset(warm_in[:], 0.0)
        nc.scalar.activation(out=warm_out[:], in_=warm_in[:], func=ACT.Exp)

        w_bf16 = const.tile([P, PACK], BF16)
        b0_bf16 = const.tile([P, B, PACK], BF16)
        nc.scalar.dma_start(out=w_bf16[:], in_=w.rearrange("(p t) -> p t", t=PACK))
        nc.scalar.dma_start(out=b0_bf16[:], in_=b0.rearrange("b (p t) -> p b t", t=PACK))

        rows = const.tile([P, C], BF16)
        nc.vector.memset(rows[:], 0.0)
        nc.scalar.dma_start(out=rows[ROW_XPREV : ROW_XPREV + B, :], in_=x_prev0)
        nc.sync.dma_start(out=rows[ROW_A0 : ROW_A0 + B, :], in_=a0)
        for queue, row, vector in (
            (nc.sync, ROW_MU, mu_r),
            (nc.scalar, ROW_MU + 1, mu_k),
            (nc.sync, ROW_MU + 2, mu_v),
            (nc.scalar, ROW_U, u),
        ):
            queue.dma_start(out=rows[row : row + 1, :], in_=vector.unsqueeze(0))

        load_x(1, nc.scalar)

        arrived_codes = const.tile([P, 4, PACK * C], U8, align_bytes=64)
        arrived_planes = const.tile([P, 4, C], U8, align_bytes=64)
        nc.vector.memset(arrived_planes[:].rearrange("p w n -> p (w n)").bitcast(I32), 0)
        weights = (
            (W_r_words, W_r_scales),
            (W_k_words, W_k_scales),
            (W_v_words, W_v_scales),
            (W_out_words, W_out_scales),
        )
        for wi, (words, scales) in enumerate(weights):
            nc.sync.dma_start(
                out=arrived_codes[:, wi, :].bitcast(I32),
                in_=words[0].rearrange("p n t -> p (n t)").bitcast(I32),
            )
            for quadrant in range(4):
                nc.sync.dma_start(
                    out=arrived_planes[32 * quadrant : 32 * quadrant + 4, wi, :].bitcast(I32),
                    in_=scales[0, 4 * quadrant : 4 * quadrant + 4, :].bitcast(I32),
                )

        w_codes = const.tile([P, 3, PACK * C], U8, align_bytes=64)
        w_planes = const.tile([P, 3, C], U8, align_bytes=64)

        def move_codes(wi):
            nc.gpsimd.tensor_copy(
                out=w_codes[:, wi, :].bitcast(I32).rearrange("p (t m) -> p t m", t=PACK),
                in_=arrived_codes[:, wi, :].bitcast(I32).rearrange("p (m t) -> p t m", t=PACK),
            )

        def move_scales(wi):
            nc.gpsimd.tensor_copy(
                out=w_planes[:, wi, :].rearrange("p (t m) -> p t m", t=PACK),
                in_=arrived_planes[:, wi, :].rearrange("p (m t) -> p t m", t=PACK),
            )

        ident_bf16 = const.tile([P, P], BF16)
        make_identity(nc, ident_bf16[:])
        ident_f32 = const.tile([P, P], F32)
        make_identity(nc, ident_f32[:])

        difference = const.tile([P, P], BF16)
        nc.vector.tensor_copy(out=difference[:], in_=ident_bf16[:])
        nc.vector.tensor_sub(out=difference[:, 1:P], in0=difference[:, 1:P], in1=ident_bf16[:, 0 : P - 1])
        neg_ident = const.tile([P, P], BF16)
        nc.vector.tensor_scalar_mul(out=neg_ident[:], in0=ident_bf16[:], scalar1=-1.0)

        counts_i32 = back.tile([P, T], I32, tag="o_sb", bufs=4)
        nc.gpsimd.iota(counts_i32[:], pattern=[[1, T]], base=1, channel_multiplier=0)
        counts = const.tile([P, T], F32)
        nc.vector.tensor_copy(out=counts[:], in_=counts_i32[:])
        eps_col = const.tile([P, 1], F32)
        nc.vector.memset(eps_col[:], EPS)

        cols = const.tile([P, PACK, ROWS], F32)
        a0_col = cols[:, :, ROW_A0 : ROW_A0 + B]
        b0_col = const.tile([P, PACK, B], F32)
        neg_w = const.tile([P, PACK], F32)
        neg_u = const.tile([P, PACK], F32)
        chi_bias = const.tile([P, PACK, B], F32)
        neg_alpha = const.tile([P, PACK, B], F32)
        b0_inverse = const.tile([P, PACK, B], F32)
        ln_beta = const.tile([P, B, PACK, T], F32)
        decay = back.tile([P, PACK, T], F32, tag="r_planes", bufs=3)
        nc.vector.tensor_scalar_mul(out=neg_w[:], in0=w_bf16[:], scalar1=-1.0)
        nc.vector.tensor_copy(out=b0_col[:], in_=b0_bf16[:].rearrange("p b t -> p t b"))
        for t in range(PACK):
            nc.scalar.activation(out=decay[:, t, :], in_=counts[:], func=ACT.Exp, scale=neg_w[:, t : t + 1])
        nc.scalar.activation(out=chi_bias[:], in_=b0_col[:], func=ACT.Ln, scale=1.0 / EPS)
        nc.vector.reciprocal(b0_inverse[:], b0_col[:])

        for wi in (W_R, W_K, W_V):
            move_codes(wi)
        move_scales(W_R)
        move_scales(W_K)

        def per_channel_numbers():
            rows_t = psum.tile([P, PACK, P], BF16, tag="o")
            for t in range(PACK):
                nc.tensor.transpose(rows_t[:, t, :], rows[:, t:C:PACK], ident_bf16[:])
            nc.vector.tensor_copy(out=cols[:], in_=rows_t[:, :, 0:ROWS])
            nc.vector.tensor_scalar_mul(out=neg_u[:], in0=cols[:, :, ROW_U], scalar1=-1.0)
            nc.vector.scalar_tensor_tensor(
                out=neg_alpha[:], in0=a0_col, scalar=-1.0, in1=b0_inverse[:], op0=ALU.mult, op1=ALU.mult
            )

        def make_ln_beta(q):
            for t in range(PACK):
                nc.scalar.activation(
                    out=ln_beta[:, q, t, :],
                    in_=decay[:, t, :],
                    func=ACT.Ln,
                    scale=b0_col[:, t, q : q + 1],
                    bias=eps_col[:],
                )

        x_pairs, steps, mixed_planes, mixed, mixes = {}, {}, {}, {}, {}

        def copy(on_vector, dst, src):
            if on_vector:
                nc.vector.tensor_copy(out=dst, in_=src)
            else:
                nc.scalar.copy(out=dst, in_=src)

        def transpose_x(f, pair, on_vector):
            if pair == 0:
                x_pairs[f] = front.tile([P, 2, T + 1], F32, tag="x_pairs", name="x_pairs")
            else:
                copy(
                    on_vector,
                    x_pairs[f][:].rearrange("p u k -> p (u k)").bitcast(BF16).rearrange(
                        "p (u k e) -> p u k e", u=2, e=2
                    )[:, :, 0, :],
                    cols[:, :, ROW_XPREV + f].rearrange("p (u e) -> p u e", e=2),
                )
            xt = psum.tile([P, T], F32, tag="xt")
            for i in range(TOK_TILES):
                nc.tensor.transpose(
                    xt[:, P * i : P * (i + 1)],
                    x_rows[f][:, i, :].bitcast(F32)[:, pair : C // 2 : 2],
                    ident_f32[:],
                )
            copy(on_vector, x_pairs[f][:, pair, 1 : T + 1], xt[:])

        def difference_plane(f, t):
            steps[f, t] = psum.tile([P, T], F32, tag=FRONT_BANKS[t % 2], name="step")
            for i in range(TOK_TILES):
                nc.tensor.matmul(
                    out=steps[f, t][:, P * i : P * (i + 1)],
                    lhsT=x_rows[f][:, i, t:C:PACK],
                    rhs=difference[:],
                    start=True,
                    stop=False,
                )
                if i == 0:
                    before, row = rows, ROW_XPREV + f
                else:
                    before, row = x_rows[f][:, i - 1, :], P - 1
                nc.tensor.matmul(
                    out=steps[f, t][:, P * i : P * i + 1],
                    lhsT=before[:, t:C:PACK],
                    rhs=neg_ident[:, row : row + 1],
                    start=False,
                    stop=True,
                )

        def mix_plane(f, t):
            for mix in MIX_ORDER:
                if t == 0:
                    mixed_planes[f, mix] = front.tile(
                        [P, PACK, T], BF16, tag="mixed_planes%d" % mix, name="mixed_planes"
                    )
                nc.vector.scalar_tensor_tensor(
                    out=mixed_planes[f, mix][:, t, :],
                    in0=steps[f, t][:],
                    scalar=cols[:, t, ROW_MU + mix : ROW_MU + mix + 1],
                    in1=x_pairs[f][:, t // 2, 0:T].bitcast(BF16)[:, t % 2 : 2 * T : 2],
                    op0=ALU.mult,
                    op1=ALU.add,
                )

        def regroup_mix(f, mix, on_gpsimd):
            if on_gpsimd:
                mixed[f, mix] = front.tile([P, T, PACK], BF16, tag="mixed_early", name="mixed", bufs=1, align_bytes=64)
                nc.gpsimd.tensor_scalar(
                    out=mixed[f, mix][:],
                    in0=mixed_planes[f, mix][:].rearrange("p t k -> p k t"),
                    scalar1=1.0,
                    scalar2=0.0,
                    op0=ALU.mult,
                    op1=ALU.add,
                )
            else:
                mixed[f, mix] = front.tile([P, T, PACK], BF16, tag="mixed", name="mixed", align_bytes=64)
                nc.scalar.copy(
                    out=mixed[f, mix][:].rearrange("p (c i) t -> p c t i", i=4),
                    in_=mixed_planes[f, mix][:].rearrange("p t (c i) -> p c t i", i=4),
                )

        def quantise_mix(f, mix):
            codes = front.tile([P, T], U32, tag="codes%d" % mix, align_bytes=64)
            plane = front.tile([P, T], U8, tag="plane%d" % mix, align_bytes=64)
            nc.vector.quantize_mx(
                out=codes[:].bitcast(FP8X4),
                scales=plane[:],
                in_=mixed[f, mix][:].rearrange("p k t -> p (k t)"),
            )
            mixes[f, mix] = (codes, plane)

        acc, chi, logit, ns, r_planes, bracket, ns_bracket, wkv_planes = {}, {}, {}, {}, {}, {}, {}, {}

        def stage1(n, which):
            b, t = divmod(n, PACK)
            codes, plane = mixes[b, which]
            acc[n, which] = psum.tile([P, T], F32, tag="acc%d" % which, name="acc", bufs=3 if which == W_V else 1)
            nc.tensor.matmul_mx(
                out=acc[n, which][:],
                lhsT=w_codes[:, which, PACK * P * t : PACK * P * (t + 1)].bitcast(FP8X4),
                lhsT_scale=w_planes[:, which, P * t : P * (t + 1)],
                rhs=codes[:].bitcast(FP8X4),
                rhs_scale=plane[:],
                start=True,
                stop=True,
            )

        def gates_without_k(n):
            b, t = divmod(n, PACK)
            chi[n] = back.tile([P, T], F32, tag="chi", name="chi")
            nc.scalar.activation(
                out=chi[n][:],
                in_=counts[:],
                func=ACT.Sigmoid,
                scale=neg_w[:, t : t + 1],
                bias=chi_bias[:, t, b : b + 1],
            )
            if t == 0:
                r_planes[b] = back.tile([P, PACK, T], F32, tag="r_planes", name="r_planes", bufs=3)
            nc.scalar.activation(out=r_planes[b][:, t, :], in_=acc[n, W_R][:], func=ACT.Sigmoid)

        def make_logit(n):
            b, t = divmod(n, PACK)
            logit[n] = back.tile([P, T], F32, tag="logit", name="logit")
            nc.vector.tensor_sub(out=logit[n][:], in0=acc[n, W_K][:], in1=ln_beta[:, b, t, :])

        def gate_ns(n):
            t = n % PACK
            ns[n] = back.tile([P, T], F32, tag="ns", name="ns")
            nc.scalar.activation(
                out=ns[n][:], in_=logit[n][:], func=ACT.Sigmoid, scale=-1.0, bias=neg_u[:, t : t + 1]
            )

        def make_bracket(n):
            b, t = divmod(n, PACK)
            bracket[n] = back.tile([P, T], F32, tag="bracket", name="bracket")
            nc.vector.scalar_tensor_tensor(
                out=bracket[n][:],
                in0=chi[n][:],
                scalar=neg_alpha[:, t, b : b + 1],
                in1=acc[n, W_V][:],
                op0=ALU.mult,
                op1=ALU.add,
            )
            ns_bracket[n] = back.tile([P, T], F32, tag="ns_bracket", name="ns_bracket")
            engine = nc.vector if n == UNITS - 1 else nc.gpsimd
            engine.tensor_mul(out=ns_bracket[n][:], in0=bracket[n][:], in1=ns[n][:])

        def make_wkv(n):
            b, t = divmod(n, PACK)
            if t == 0:
                wkv_planes[b] = back.tile([P, PACK, T], F32, tag="wkv_planes", name="wkv_planes")
            nc.vector.tensor_sub(out=wkv_planes[b][:, t, :], in0=acc[n, W_V][:], in1=ns_bracket[n][:])

        h_words, h_mx = {}, {}

        def make_h(g, i, on_vector):
            if on_vector:
                h_words[g, i] = back.tile([P, P, PACK], BF16, tag="h_words_late", name="h_words", align_bytes=64)
            else:
                h_words[g, i] = back.tile([P, P, PACK], BF16, tag="h_words", name="h_words", bufs=1, align_bytes=64)
            engine = nc.vector if on_vector else nc.gpsimd
            engine.tensor_mul(
                out=h_words[g, i][:].rearrange("p (c i) t -> p c t i", i=4),
                in0=wkv_planes[g][:, :, P * i : P * (i + 1)].rearrange("p t (c i) -> p c t i", i=4),
                in1=r_planes[g][:, :, P * i : P * (i + 1)].rearrange("p t (c i) -> p c t i", i=4),
            )

        def quantise_h(g, i):
            codes = back.tile([P, P], U32, tag="h_codes", bufs=HELD_SLICES, align_bytes=64)
            plane = back.tile([P, P], U8, tag="h_plane", bufs=HELD_SLICES, align_bytes=64)
            nc.vector.quantize_mx(
                out=codes[:].bitcast(FP8X4),
                scales=plane[:],
                in_=h_words[g, i][:].rearrange("p k t -> p (k t)"),
            )
            h_mx[g, i] = (codes, plane)

        o_accs = {}

        def project(g, i, bank):
            codes, plane = h_mx[g, i]
            o_accs[g, i] = psum.tile([P, C], F32, tag=bank, name="o_acc")
            nc.tensor.matmul_mx(
                out=o_accs[g, i][:],
                lhsT=codes[:].bitcast(FP8X4),
                lhsT_scale=plane[:],
                rhs=arrived_codes[:, W_OUT, :].bitcast(FP8X4),
                rhs_scale=arrived_planes[:, W_OUT, :],
                start=True,
                stop=True,
            )

        def store(g, i, on_vector, borrowed):
            if borrowed is None:
                o_sb = back.tile([P, C], F32, tag="o_sb", bufs=4)
            else:
                o_sb = front.tile([P, C], F32, tag="mixed_planes%d" % borrowed, name="o_sb")
            copy(on_vector, o_sb[:], o_accs[g, i][:])
            nc.sync.dma_start(out=out[g, P * i : P * (i + 1), :], in_=o_sb[:])

        def is_sequence(q):
            return 0 <= q < B

        def is_unit(n):
            return 0 <= n < UNITS

        quantised = []
        projected = 0
        in_psum = []
        stored = 0

        for n in range(FIRST_STEP, LAST_STEP):
            warming_up = n < 0
            after_gpsimd = n + QUANTISE_LEAD - REGROUP_LEAD < 0
            mixing = n <= LAST_MIX_STEP
            cooling_down = n >= UNITS

            f, part = divmod(n + LOAD_LEAD, PACK)
            if is_sequence(f) and part == 0 and f >= LOADED_AT_START:
                load_x(f, nc.sync)

            f, part = divmod(n + QUANTISE_LEAD, PACK)
            if is_sequence(f) and part < 3 and not after_gpsimd:
                quantise_mix(f, MIX_ORDER[part])
            h_on_vector = not mixing
            f, part = divmod(n - H_LAG, TOK_TILES)
            if is_sequence(f) and h_on_vector:
                make_h(f, part, True)
            f, part = divmod(n - QUANTISE_H_LAG, TOK_TILES)
            if is_sequence(f):
                quantise_h(f, part)
                quantised.append((f, part))
            f, part = divmod(n - H_LAG, TOK_TILES)
            if is_sequence(f) and not h_on_vector:
                make_h(f, part, False)

            if is_unit(n + 1):
                stage1(n + 1, W_K)
                stage1(n + 1, W_R)
                stage1(n + 1, W_V)
            if is_unit(n):
                make_bracket(n)
            if is_unit(n - WKV_LAG):
                make_wkv(n - WKV_LAG)

            f, part = divmod(n + REGROUP_LEAD, PACK)
            if is_sequence(f) and part < 3 and (part == 0 or not warming_up):
                regroup_mix(f, MIX_ORDER[part], warming_up)
            if is_unit(n + 1):
                gates_without_k(n + 1)

            for k, (g, i) in enumerate(in_psum):
                full = len(in_psum) == len(FRONT_BANKS)
                on_vector = n <= LAST_REGROUP_STEP or (k == 0 and full) or n == LAST_STEP - 1
                if n > LAST_REGROUP_STEP and stored % 2 == 1:
                    store(g, i, on_vector, MIX_ORDER[stored // 2 % len(MIX_ORDER)])
                else:
                    store(g, i, on_vector, None)
                stored += 1
            if mixing:
                due = 0
            elif n < LAST_REGROUP_STEP:
                due = 2
            else:
                due = len(FRONT_BANKS)
            in_psum = quantised[projected : projected + due]
            for k, (g, i) in enumerate(in_psum):
                project(g, i, FRONT_BANKS[(projected + k) % len(FRONT_BANKS)])
            projected += len(in_psum)

            f, part = divmod(n + TRANSPOSE_LEAD, PACK)
            if is_sequence(f) and part < 2:
                transpose_x(f, part, f <= 1)
            if n == FIRST_STEP:
                per_channel_numbers()
            f, part = divmod(n + MIX_LEAD, PACK)
            if is_sequence(f):
                mix_plane(f, part)
            f, part = divmod(n + DIFFERENCE_LEAD, PACK)
            if is_sequence(f):
                difference_plane(f, part)

            f, part = divmod(n + QUANTISE_LEAD, PACK)
            if is_sequence(f) and part < 3 and after_gpsimd:
                quantise_mix(f, MIX_ORDER[part])
            f, part = divmod(n + REGROUP_LEAD, PACK)
            if is_sequence(f) and 0 < part < 3 and warming_up:
                regroup_mix(f, MIX_ORDER[part], True)
            if n == LAST_MOVE_STEP:
                move_scales(W_V)

            if is_unit(n + 1):
                make_logit(n + 1)
                gate_ns(n + 1)
            if is_sequence(n + LN_BETA_LEAD):
                make_ln_beta(n + LN_BETA_LEAD)
